import numpy as np
import ml_dtypes


def mxq(x, axis, fmt="e4m3"):
    dtype, down = {"e4m3": (ml_dtypes.float8_e4m3fn, 7), "e5m2": (ml_dtypes.float8_e5m2, 14)}[fmt]
    v = np.moveaxis(np.asarray(x, np.float32).astype(ml_dtypes.bfloat16).astype(np.float64), axis, -1)
    blocks = v.reshape(v.shape[:-1] + (-1, 32))
    amax = np.abs(blocks).max(-1, keepdims=True)
    byte = np.maximum(np.where(amax > 0, np.frexp(amax)[1] - 1 + 127, 0) - down, 1)
    scale = np.exp2(byte - 127.0)
    codes = (blocks / scale).astype(np.float32).astype(dtype).astype(np.float64)
    return np.moveaxis((codes * scale).reshape(v.shape), -1, axis)


WIDE = False


def mx_kscale(k):
    if not WIDE:
        return np.ones(k)
    levels = np.array([10, -10, 5, -5, 0])
    if k % 512:
        return np.exp2(np.random.permutation(np.resize(levels, k // 32))).repeat(32)
    a = np.empty((k // 512, 16))
    for p in range(k // 512):
        a[p, :8] = np.random.permutation(np.resize(levels, 8))
        for g in range(8):
            far = levels[np.abs(levels - a[p, g]) >= 10]
            a[p, g + 8] = far[np.random.randint(len(far))]
    return np.exp2(a.ravel()).repeat(32)


BF16 = ml_dtypes.bfloat16


def bf(x):
    return np.asarray(x, np.float32).astype(BF16)


def f64(x):
    return np.asarray(x).astype(np.float64)


B, S, H = 8, 129, 1024
N = B * (S - 1)
G = 0.75


def setup_inputs():
    s = mx_kscale(H)
    return {"x": bf(np.random.standard_normal((B, S, H)) * s),
            "k1": bf(np.random.standard_normal((N, H)) * G * s),
            "k2": bf(np.random.standard_normal((N, H)) * G * np.sqrt(1.0 + 0.25 * G * G) * s),
            "coefficients": bf(np.random.standard_normal((H, H)) * G / np.sqrt(H) * s[:, None] / s[None, :])}


def reference(x, k1, k2, coefficients):
    x, k1, k2 = f64(x), f64(k1), f64(k2)
    y = x[:, :-1, :].reshape(-1, H)
    cq = mxq(f64(coefficients), 1, "e4m3")
    k3 = mxq(y + 0.5 * k2, 1, "e4m3") @ cq.T
    k4 = mxq(y + k3, 1, "e4m3") @ cq.T
    y1 = y + (k1 + 2.0 * k2 + 2.0 * k3 + k4) / 6.0
    return y1.reshape(B, S - 1, H) - x[:, 1:, :]

@@ -1,0 +1,216 @@
+from contextlib import ExitStack
+
+import concourse.mybir as mybir
+from concourse.masks import make_identity
+
+BF16 = mybir.dt.bfloat16
+F32 = mybir.dt.float32
+U32 = mybir.dt.uint32
+U8 = mybir.dt.uint8
+FP8X4 = mybir.dt.float8_e4m3fn_x4
+ADD = mybir.AluOpType.add
+SUBTRACT = mybir.AluOpType.subtract
+MULT = mybir.AluOpType.mult
+COPY = mybir.ActivationFunctionType.Copy
+
+P = 128
+PACK = 4
+PAIR = 2
+K_PASS = P * PACK
+H = 1024
+PASSES = H // K_PASS
+BANK = 512
+HALVES = H // BANK
+ROW_TILES = 8
+
+AHEAD = 2
+
+FLOPS = 2 * 2 * (ROW_TILES * P) * H * H
+
+
+def tile_sindylossmixin_pa_kernel(tc, x, k1, k2, coefficients, out):
+    nc = tc.nc
+    with ExitStack() as stack:
+        stack.enter_context(tc.manual_schedule())
+        keep = stack.enter_context(tc.tile_pool(name="keep", bufs=1))
+        work = stack.enter_context(tc.tile_pool(name="work", bufs=3))
+        turned_banks = stack.enter_context(tc.psum_pool(name="turned_banks", bufs=4))
+        product_banks = stack.enter_context(tc.psum_pool(name="product_banks", bufs=4))
+
+        identity = keep.tile([P, P], F32)
+        make_identity(nc, identity[:])
+
+        y, x_next, k1_rows, k2_rows, c_rows = [], [], [], [], []
+        for t in range(ROW_TILES):
+            y.append(keep.tile([P, H], BF16, name="y%d" % t))
+            x_next.append(keep.tile([P, H], BF16, name="x_next%d" % t))
+            k1_rows.append(keep.tile([P, H], BF16, name="k1_rows%d" % t))
+            k2_rows.append(keep.tile([P, H], BF16, name="k2_rows%d" % t))
+            c_rows.append(keep.tile([P, H], BF16, name="c_rows%d" % t))
+
+        def load_first_argument(t):
+            nc.sync.dma_start(out=y[t][:], in_=x[t, 0:P, :])
+            nc.sync.dma_start(out=k2_rows[t][:], in_=k2[t * P : (t + 1) * P, :])
+
+        def load_rest(t):
+            nc.sync.dma_start(out=k1_rows[t][:], in_=k1[t * P : (t + 1) * P, :])
+            nc.sync.dma_start(out=x_next[t][:], in_=x[t, 1 : P + 1, :])
+
+        load_first_argument(0)
+        for r in range(ROW_TILES):
+            nc.sync.dma_start(out=c_rows[r][:], in_=coefficients[r * P : (r + 1) * P, :])
+        for t in range(1, ROW_TILES):
+            load_first_argument(t)
+            load_rest(t - 1)
+        load_rest(ROW_TILES - 1)
+
+        c_grouped = keep.tile([P, PASSES, H, PAIR], F32, align_bytes=64)
+        c_codes = keep.tile([P, PASSES, H], U32, align_bytes=64)
+        c_scales = keep.tile([P, PASSES, H], U8, align_bytes=64)
+        tiles_per_half = BANK // P
+
+        def prepare_coefficients():
+            for r in range(ROW_TILES):
+                rows = slice(r * P, (r + 1) * P)
+                words = c_rows[r][:].bitcast(F32)
+                turned = turned_banks.tile([P, PASSES, PAIR, P], F32, tag="turned")
+                for g in range(PASSES):
+                    for u in range(PAIR):
+                        first = g * PAIR * P + u
+                        nc.tensor.transpose(
+                            turned[:, g, u, :], words[:, first : (g + 1) * PAIR * P : PAIR], identity[:]
+                        )
+                copy_out = nc.vector.tensor_copy if r % 2 == 0 else nc.scalar.copy
+                copy_out(out=c_grouped[:, :, rows, :], in_=turned[:].rearrange("p g u i -> p g i u"))
+                if (r + 1) % tiles_per_half == 0:
+                    half = slice((r + 1) * P - BANK, (r + 1) * P)
+                    for g in range(PASSES):
+                        nc.vector.quantize_mx(
+                            out=c_codes[:, g, half].bitcast(FP8X4),
+                            scales=c_scales[:, g, half],
+                            in_=c_grouped[:, g, half, :].rearrange("p i u -> p (i u)").bitcast(BF16),
+                        )
+
+        doubled_a, b, b_plus_a, total = {}, {}, {}, {}
+        grouped, quantised, product = {}, {}, {}
+
+        def turn(label, argument, scale, t):
+            grouped[label, t] = work.tile(
+                [P, PASSES, P, PACK], BF16, name="grouped_" + label, align_bytes=64
+            )
+            columns = argument[:].rearrange("n (g q j) -> n g j q", g=PASSES, q=P, j=PACK)
+            for g in range(PASSES):
+                turned = turned_banks.tile([P, PACK, P], F32, tag="turned")
+                for j in range(PACK):
+                    nc.tensor.transpose(turned[:, j, :], columns[:, g, j, :], identity[:])
+                nc.scalar.activation(
+                    out=grouped[label, t][:, g, :, :],
+                    in_=turned[:].rearrange("p j n -> p n j"),
+                    func=COPY,
+                    scale=scale,
+                )
+
+        def first_argument(t):
+            doubled_a[t] = work.tile([P, H], F32, name="doubled_a", bufs=AHEAD + 2)
+            nc.vector.scalar_tensor_tensor(
+                out=doubled_a[t][:], in0=y[t][:], scalar=2.0, in1=k2_rows[t][:], op0=MULT, op1=ADD
+            )
+            turn("a", doubled_a[t], 0.5, t)
+
+        def quantise(label, t):
+            codes = work.tile([P, PASSES, P], U32, name="codes_" + label, align_bytes=64)
+            scales = work.tile([P, PASSES, P], U8, name="scales_" + label, align_bytes=64)
+            nc.vector.quantize_mx(
+                out=codes[:].rearrange("p g n -> p (g n)").bitcast(FP8X4),
+                scales=scales[:].rearrange("p g n -> p (g n)"),
+                in_=grouped[label, t][:].rearrange("p g n j -> p (g n j)"),
+            )
+            quantised[label, t] = (codes, scales)
+
+        def times_coefficients(label, t):
+            codes, scales = quantised[label, t]
+            for h in range(HALVES):
+                cols = slice(h * BANK, (h + 1) * BANK)
+                product[label, t, h] = product_banks.tile([P, BANK], F32, name="product")
+                for g in range(PASSES):
+                    nc.tensor.matmul_mx(
+                        out=product[label, t, h][:],
+                        lhsT=codes[:, g, :].bitcast(FP8X4),
+                        lhsT_scale=scales[:, g, :],
+                        rhs=c_codes[:, g, cols].bitcast(FP8X4),
+                        rhs_scale=c_scales[:, g, cols],
+                        start=(g == 0),
+                        stop=(g == PASSES - 1),
+                    )
+
+        def compute_second_argument(t):
+            b[t] = work.tile([P, H], F32, name="b")
+            for h in range(HALVES):
+                cols = slice(h * BANK, (h + 1) * BANK)
+                k3 = product["a", t, h]
+                nc.vector.tensor_tensor(out=b[t][:, cols], in0=k3[:], in1=y[t][:, cols], op=ADD)
+
+        def add_arguments(t):
+            b_plus_a[t] = work.tile([P, H], F32, name="b_plus_a")
+            nc.vector.tensor_tensor(out=b_plus_a[t][:], in0=b[t][:], in1=doubled_a[t][:], op=ADD)
+
+        def start_total(t):
+            total[t] = work.tile([P, H], F32, name="total", bufs=5)
+            nc.scalar.activation(out=total[t][:], in_=k1_rows[t][:], func=COPY, scale=1.0 / 6.0)
+
+        def subtract_next_state(t):
+            nc.gpsimd.tensor_tensor(
+                out=total[t][:], in0=total[t][:], in1=x_next[t][:], op=SUBTRACT
+            )
+
+        def add_arguments_to_total(t):
+            nc.vector.scalar_tensor_tensor(
+                out=total[t][:],
+                in0=b_plus_a[t][:],
+                scalar=1.0 / 3.0,
+                in1=total[t][:],
+                op0=MULT,
+                op1=ADD,
+            )
+
+        def add_k4_and_store(t):
+            for h in range(HALVES):
+                cols = slice(h * BANK, (h + 1) * BANK)
+                k4 = product["b", t, h]
+                nc.vector.scalar_tensor_tensor(
+                    out=total[t][:, cols],
+                    in0=k4[:],
+                    scalar=1.0 / 6.0,
+                    in1=total[t][:, cols],
+                    op0=MULT,
+                    op1=ADD,
+                )
+                nc.sync.dma_start(out=out[t, :, cols], in_=total[t][:, cols])
+
+        def exists(t):
+            return 0 <= t < ROW_TILES
+
+        first_argument(0)
+        prepare_coefficients()
+        for r in range(1 - AHEAD, ROW_TILES + 1):
+            if exists(r):
+                subtract_next_state(r)
+            if exists(r):
+                compute_second_argument(r)
+            if exists(r - 1):
+                add_k4_and_store(r - 1)
+            if exists(r):
+                turn("b", b[r], 1.0, r)
+            if exists(r + 1):
+                start_total(r + 1)
+            if exists(r + 1):
+                quantise("a", r + 1)
+                times_coefficients("a", r + 1)
+            if exists(r):
+                add_arguments(r)
+                quantise("b", r)
+                times_coefficients("b", r)
+            if exists(r + AHEAD):
+                first_argument(r + AHEAD)
+            if exists(r):
+                add_arguments_to_total(r)

@@ -22,8 +22,7 @@ PASSES = H // K_PASS
 BANK = 512
 HALVES = H // BANK
 ROW_TILES = 8
-
-AHEAD = 2
+WORDS = K_PASS // PAIR
 
 FLOPS = 2 * 2 * (ROW_TILES * P) * H * H
 
@@ -34,8 +33,9 @@ def tile_sindylossmixin_pa_kernel(tc, x, k1, k2, coefficients, out):
         stack.enter_context(tc.manual_schedule())
         keep = stack.enter_context(tc.tile_pool(name="keep", bufs=1))
         work = stack.enter_context(tc.tile_pool(name="work", bufs=3))
-        turned_banks = stack.enter_context(tc.psum_pool(name="turned_banks", bufs=4))
-        product_banks = stack.enter_context(tc.psum_pool(name="product_banks", bufs=4))
+        turned_banks = stack.enter_context(tc.psum_pool(name="turned_banks", bufs=2))
+        k3_banks = stack.enter_context(tc.psum_pool(name="k3_banks", bufs=2))
+        sum_banks = stack.enter_context(tc.psum_pool(name="sum_banks", bufs=4))
 
         identity = keep.tile([P, P], F32)
         make_identity(nc, identity[:])
@@ -56,9 +56,10 @@ def tile_sindylossmixin_pa_kernel(tc, x, k1, k2, coefficients, out):
             nc.sync.dma_start(out=k1_rows[t][:], in_=k1[t * P : (t + 1) * P, :])
             nc.sync.dma_start(out=x_next[t][:], in_=x[t, 1 : P + 1, :])
 
+        c_by_slot = coefficients.rearrange("(b m j) k -> b j m k", b=HALVES, j=PACK)
         load_first_argument(0)
-        for r in range(ROW_TILES):
-            nc.sync.dma_start(out=c_rows[r][:], in_=coefficients[r * P : (r + 1) * P, :])
+        for s in range(ROW_TILES):
+            nc.sync.dma_start(out=c_rows[s][:], in_=c_by_slot[s // PACK, s % PACK])
         for t in range(1, ROW_TILES):
             load_first_argument(t)
             load_rest(t - 1)
@@ -67,95 +68,149 @@ def tile_sindylossmixin_pa_kernel(tc, x, k1, k2, coefficients, out):
         c_grouped = keep.tile([P, PASSES, H, PAIR], F32, align_bytes=64)
         c_codes = keep.tile([P, PASSES, H], U32, align_bytes=64)
         c_scales = keep.tile([P, PASSES, H], U8, align_bytes=64)
-        tiles_per_half = BANK // P
 
-        def prepare_coefficients():
-            for r in range(ROW_TILES):
-                rows = slice(r * P, (r + 1) * P)
-                words = c_rows[r][:].bitcast(F32)
-                turned = turned_banks.tile([P, PASSES, PAIR, P], F32, tag="turned")
-                for g in range(PASSES):
-                    for u in range(PAIR):
-                        first = g * PAIR * P + u
-                        nc.tensor.transpose(
-                            turned[:, g, u, :], words[:, first : (g + 1) * PAIR * P : PAIR], identity[:]
-                        )
-                copy_out = nc.vector.tensor_copy if r % 2 == 0 else nc.scalar.copy
-                copy_out(out=c_grouped[:, :, rows, :], in_=turned[:].rearrange("p g u i -> p g i u"))
-                if (r + 1) % tiles_per_half == 0:
-                    half = slice((r + 1) * P - BANK, (r + 1) * P)
-                    for g in range(PASSES):
-                        nc.vector.quantize_mx(
-                            out=c_codes[:, g, half].bitcast(FP8X4),
-                            scales=c_scales[:, g, half],
-                            in_=c_grouped[:, g, half, :].rearrange("p i u -> p (i u)").bitcast(BF16),
-                        )
-
-        doubled_a, b, b_plus_a, total = {}, {}, {}, {}
-        grouped, quantised, product = {}, {}, {}
-
-        def turn(label, argument, scale, t):
-            grouped[label, t] = work.tile(
-                [P, PASSES, P, PACK], BF16, name="grouped_" + label, align_bytes=64
-            )
-            columns = argument[:].rearrange("n (g q j) -> n g j q", g=PASSES, q=P, j=PACK)
+        def turn_words(turned, rows):
+            words = rows[:].bitcast(F32)
             for g in range(PASSES):
-                turned = turned_banks.tile([P, PACK, P], F32, tag="turned")
-                for j in range(PACK):
-                    nc.tensor.transpose(turned[:, j, :], columns[:, g, j, :], identity[:])
-                nc.scalar.activation(
-                    out=grouped[label, t][:, g, :, :],
-                    in_=turned[:].rearrange("p j n -> p n j"),
-                    func=COPY,
-                    scale=scale,
+                for u in range(PAIR):
+                    nc.tensor.transpose(
+                        turned[:, g, u, :],
+                        words[:, g * WORDS + u : (g + 1) * WORDS : PAIR],
+                        identity[:],
+                    )
+
+        def prepare_coefficients(s):
+            pool = (turned_banks, turned_banks, k3_banks, k3_banks)[s] if s < 4 else sum_banks
+            label = ("turned", "turned", "k3", "k3")[s] if s < 4 else "total_sum"
+            turned = pool.tile([P, PASSES, PAIR, P], F32, name=label)
+            turn_words(turned, c_rows[s])
+            copy_out = nc.vector.tensor_copy if s % 2 == 0 else nc.scalar.copy
+            copy_out(
+                out=c_grouped[:, :, s * P : (s + 1) * P, :],
+                in_=turned[:].rearrange("p g u i -> p g i u"),
+            )
+
+        def quantise_coefficients(b):
+            half = slice(b * BANK, (b + 1) * BANK)
+            for g in range(PASSES):
+                nc.vector.quantize_mx(
+                    out=c_codes[:, g, half].bitcast(FP8X4),
+                    scales=c_scales[:, g, half],
+                    in_=c_grouped[:, g, half, :].rearrange("p i u -> p (i u)").bitcast(BF16),
                 )
 
-        def first_argument(t):
-            doubled_a[t] = work.tile([P, H], F32, name="doubled_a", bufs=AHEAD + 2)
-            nc.vector.scalar_tensor_tensor(
-                out=doubled_a[t][:], in0=y[t][:], scalar=2.0, in1=k2_rows[t][:], op0=MULT, op1=ADD
-            )
-            turn("a", doubled_a[t], 0.5, t)
+        doubled_y, doubled_a, turned_a, turned_y = {}, {}, {}, {}
+        a_grouped, y_grouped, b_grouped = {}, {}, {}
+        a_quantised, b_quantised = {}, {}
+        doubled_k3, total_sum, total, rest = {}, {}, {}, {}
 
-        def quantise(label, t):
-            codes = work.tile([P, PASSES, P], U32, name="codes_" + label, align_bytes=64)
-            scales = work.tile([P, PASSES, P], U8, name="scales_" + label, align_bytes=64)
+        def exists(t):
+            return 0 <= t < ROW_TILES
+
+        def double_y(t):
+            doubled_y[t] = work.tile([P, H], BF16, name="doubled_y")
+            nc.scalar.activation(out=doubled_y[t][:], in_=y[t][:], func=COPY, scale=2.0)
+
+        def first_argument(t):
+            doubled_a[t] = work.tile([P, H], BF16, name="doubled_a")
+            nc.vector.tensor_tensor(
+                out=doubled_a[t][:], in0=doubled_y[t][:], in1=k2_rows[t][:], op=ADD
+            )
+
+        def turn(t):
+            turned_a[t] = turned_banks.tile([P, PASSES, PAIR, P], F32, name="turned")
+            turn_words(turned_a[t], doubled_a[t])
+            turned_y[t] = turned_banks.tile([P, PASSES, PAIR, P], F32, name="turned")
+            turn_words(turned_y[t], y[t])
+
+        def as_words(grouped):
+            return (
+                grouped[:]
+                .rearrange("p g n j -> p (g n j)")
+                .bitcast(F32)
+                .rearrange("p (g n u) -> p g n u", g=PASSES, u=PAIR)
+            )
+
+        def copy_turned(t):
+            a_grouped[t] = work.tile([P, PASSES, P, PACK], BF16, name="a_grouped", align_bytes=64)
+            nc.scalar.copy(
+                out=as_words(a_grouped[t]), in_=turned_a[t][:].rearrange("p g u n -> p g n u")
+            )
+            y_grouped[t] = work.tile([P, PASSES, P, PACK], BF16, name="y_grouped", bufs=5)
+            nc.scalar.copy(
+                out=as_words(y_grouped[t]), in_=turned_y[t][:].rearrange("p g u n -> p g n u")
+            )
+
+        def quantise(label, grouped):
+            codes = work.tile([P, PASSES, P], U32, name="codes_" + label, align_bytes=64, bufs=4)
+            scales = work.tile([P, PASSES, P], U8, name="scales_" + label, align_bytes=64, bufs=4)
             nc.vector.quantize_mx(
                 out=codes[:].rearrange("p g n -> p (g n)").bitcast(FP8X4),
                 scales=scales[:].rearrange("p g n -> p (g n)"),
-                in_=grouped[label, t][:].rearrange("p g n j -> p (g n j)"),
+                in_=grouped[:].rearrange("p g n j -> p (g n j)"),
             )
-            quantised[label, t] = (codes, scales)
+            return codes, scales
 
-        def times_coefficients(label, t):
-            codes, scales = quantised[label, t]
-            for h in range(HALVES):
-                cols = slice(h * BANK, (h + 1) * BANK)
-                product[label, t, h] = product_banks.tile([P, BANK], F32, name="product")
+        def quantise_a(t):
+            a_quantised[t] = quantise("a", a_grouped[t])
+
+        def quantise_b(t):
+            b_quantised[t] = quantise("b", b_grouped[t])
+
+        def transposed_k3(t):
+            codes, scales = a_quantised[t]
+            for b in range(HALVES):
+                doubled_k3[t, b] = k3_banks.tile([P, PACK, P], F32, name="k3")
+                for j in range(PACK):
+                    cols = slice(b * BANK + j * P, b * BANK + (j + 1) * P)
+                    for g in range(PASSES):
+                        nc.tensor.matmul_mx(
+                            out=doubled_k3[t, b][:, j, :],
+                            lhsT=c_codes[:, g, cols].bitcast(FP8X4),
+                            lhsT_scale=c_scales[:, g, cols],
+                            rhs=codes[:, g, :].bitcast(FP8X4),
+                            rhs_scale=scales[:, g, :],
+                            start=(g == 0),
+                            stop=(g == PASSES - 1),
+                        )
+
+        def times_coefficients(t, quantised, first, last):
+            codes, scales = quantised
+            for b in range(HALVES):
+                cols = slice(b * BANK, (b + 1) * BANK)
                 for g in range(PASSES):
                     nc.tensor.matmul_mx(
-                        out=product[label, t, h][:],
+                        out=total_sum[t, b][:],
                         lhsT=codes[:, g, :].bitcast(FP8X4),
                         lhsT_scale=scales[:, g, :],
                         rhs=c_codes[:, g, cols].bitcast(FP8X4),
                         rhs_scale=c_scales[:, g, cols],
-                        start=(g == 0),
-                        stop=(g == PASSES - 1),
+                        start=(first and g == 0),
+                        stop=(last and g == PASSES - 1),
                     )
 
-        def compute_second_argument(t):
-            b[t] = work.tile([P, H], F32, name="b")
-            for h in range(HALVES):
-                cols = slice(h * BANK, (h + 1) * BANK)
-                k3 = product["a", t, h]
-                nc.vector.tensor_tensor(out=b[t][:, cols], in0=k3[:], in1=y[t][:, cols], op=ADD)
+        def open_sum(t):
+            for b in range(HALVES):
+                total_sum[t, b] = sum_banks.tile([P, BANK], F32, name="total_sum")
+            times_coefficients(t, a_quantised[t], True, False)
 
-        def add_arguments(t):
-            b_plus_a[t] = work.tile([P, H], F32, name="b_plus_a")
-            nc.vector.tensor_tensor(out=b_plus_a[t][:], in0=b[t][:], in1=doubled_a[t][:], op=ADD)
+        def close_sum(t):
+            times_coefficients(t, b_quantised[t], False, True)
+
+        def second_argument(t):
+            b_grouped[t] = work.tile([P, PASSES, P, PACK], BF16, name="b_grouped", align_bytes=64)
+            for b in range(HALVES):
+                nc.vector.scalar_tensor_tensor(
+                    out=b_grouped[t][:, b, :, :],
+                    in0=doubled_k3[t, b][:].rearrange("p j n -> p n j"),
+                    scalar=0.5,
+                    in1=y_grouped[t][:, b, :, :],
+                    op0=MULT,
+                    op1=ADD,
+                )
 
         def start_total(t):
-            total[t] = work.tile([P, H], F32, name="total", bufs=5)
+            total[t] = work.tile([P, H], F32, name="total", bufs=6)
             nc.scalar.activation(out=total[t][:], in_=k1_rows[t][:], func=COPY, scale=1.0 / 6.0)
 
         def subtract_next_state(t):
@@ -163,54 +218,69 @@ def tile_sindylossmixin_pa_kernel(tc, x, k1, k2, coefficients, out):
                 out=total[t][:], in0=total[t][:], in1=x_next[t][:], op=SUBTRACT
             )
 
-        def add_arguments_to_total(t):
+        def add_y_and_k2(t):
+            rest[t] = work.tile([P, H], F32, name="rest")
             nc.vector.scalar_tensor_tensor(
-                out=total[t][:],
-                in0=b_plus_a[t][:],
-                scalar=1.0 / 3.0,
-                in1=total[t][:],
-                op0=MULT,
-                op1=ADD,
+                out=rest[t][:], in0=k2_rows[t][:], scalar=1.0 / 3.0, in1=y[t][:], op0=MULT, op1=ADD
             )
 
-        def add_k4_and_store(t):
-            for h in range(HALVES):
-                cols = slice(h * BANK, (h + 1) * BANK)
-                k4 = product["b", t, h]
+        def add_rest(t):
+            nc.vector.tensor_tensor(out=total[t][:], in0=total[t][:], in1=rest[t][:], op=ADD)
+
+        def finish(t):
+            for b in range(HALVES):
+                cols = slice(b * BANK, (b + 1) * BANK)
+                natural = total[t][:, cols].rearrange("n (m j) -> n m j", j=PACK)
                 nc.vector.scalar_tensor_tensor(
-                    out=total[t][:, cols],
-                    in0=k4[:],
+                    out=natural,
+                    in0=total_sum[t, b][:].rearrange("n (j m) -> n m j", j=PACK),
                     scalar=1.0 / 6.0,
-                    in1=total[t][:, cols],
+                    in1=natural,
                     op0=MULT,
                     op1=ADD,
                 )
                 nc.sync.dma_start(out=out[t, :, cols], in_=total[t][:, cols])
 
-        def exists(t):
-            return 0 <= t < ROW_TILES
-
+        double_y(0)
         first_argument(0)
-        prepare_coefficients()
-        for r in range(1 - AHEAD, ROW_TILES + 1):
+        for s in range(4):
+            prepare_coefficients(s)
+        quantise_coefficients(0)
+        turn(0)
+        copy_turned(0)
+        for s in range(4, 8):
+            prepare_coefficients(s)
+        quantise_a(0)
+        quantise_coefficients(1)
+        double_y(1)
+        first_argument(1)
+        start_total(0)
+
+        for r in range(-1, ROW_TILES + 1):
+            if exists(r + 1):
+                subtract_next_state(r + 1)
             if exists(r):
-                subtract_next_state(r)
-            if exists(r):
-                compute_second_argument(r)
+                second_argument(r)
             if exists(r - 1):
-                add_k4_and_store(r - 1)
-            if exists(r):
-                turn("b", b[r], 1.0, r)
+                finish(r - 1)
+            if exists(r + 2):
+                turn(r + 2)
+            if exists(r + 3):
+                double_y(r + 3)
+            if exists(r + 2):
+                copy_turned(r + 2)
             if exists(r + 1):
-                start_total(r + 1)
+                transposed_k3(r + 1)
+                open_sum(r + 1)
+            if exists(r):
+                quantise_b(r)
+                close_sum(r)
+            if exists(r + 2):
+                quantise_a(r + 2)
+            if exists(r + 3):
+                first_argument(r + 3)
+            if exists(r + 2):
+                start_total(r + 2)
             if exists(r + 1):
-                quantise("a", r + 1)
-                times_coefficients("a", r + 1)
-            if exists(r):
-                add_arguments(r)
-                quantise("b", r)
-                times_coefficients("b", r)
-            if exists(r + AHEAD):
-                first_argument(r + AHEAD)
-            if exists(r):
-                add_arguments_to_total(r)
+                add_y_and_k2(r + 1)
+                add_rest(r + 1)

@@ -102,7 +102,7 @@ def tile_sindylossmixin_pa_kernel(tc, x, k1, k2, coefficients, out):
         doubled_y, doubled_a, turned_a, turned_y = {}, {}, {}, {}
         a_grouped, y_grouped, b_grouped = {}, {}, {}
         a_quantised, b_quantised = {}, {}
-        doubled_k3, total_sum, total, rest = {}, {}, {}, {}
+        doubled_k3, total_sum, total = {}, {}, {}
 
         def exists(t):
             return 0 <= t < ROW_TILES
@@ -211,21 +211,24 @@ def tile_sindylossmixin_pa_kernel(tc, x, k1, k2, coefficients, out):
 
         def start_total(t):
             total[t] = work.tile([P, H], F32, name="total", bufs=6)
-            nc.scalar.activation(out=total[t][:], in_=k1_rows[t][:], func=COPY, scale=1.0 / 6.0)
+            nc.vector.scalar_tensor_tensor(
+                out=total[t][:], in0=k2_rows[t][:], scalar=1.0 / 3.0, in1=y[t][:], op0=MULT, op1=ADD
+            )
 
         def subtract_next_state(t):
             nc.gpsimd.tensor_tensor(
                 out=total[t][:], in0=total[t][:], in1=x_next[t][:], op=SUBTRACT
             )
 
-        def add_y_and_k2(t):
-            rest[t] = work.tile([P, H], F32, name="rest")
+        def add_k1(t):
             nc.vector.scalar_tensor_tensor(
-                out=rest[t][:], in0=k2_rows[t][:], scalar=1.0 / 3.0, in1=y[t][:], op0=MULT, op1=ADD
+                out=total[t][:],
+                in0=k1_rows[t][:],
+                scalar=1.0 / 6.0,
+                in1=total[t][:],
+                op0=MULT,
+                op1=ADD,
             )
-
-        def add_rest(t):
-            nc.vector.tensor_tensor(out=total[t][:], in0=total[t][:], in1=rest[t][:], op=ADD)
 
         def finish(t):
             for b in range(HALVES):
@@ -242,6 +245,7 @@ def tile_sindylossmixin_pa_kernel(tc, x, k1, k2, coefficients, out):
                 nc.sync.dma_start(out=out[t, :, cols], in_=total[t][:, cols])
 
         double_y(0)
+        start_total(0)
         first_argument(0)
         for s in range(4):
             prepare_coefficients(s)
@@ -252,11 +256,20 @@ def tile_sindylossmixin_pa_kernel(tc, x, k1, k2, coefficients, out):
             prepare_coefficients(s)
         quantise_a(0)
         quantise_coefficients(1)
+        transposed_k3(0)
+        open_sum(0)
         double_y(1)
         first_argument(1)
-        start_total(0)
+        subtract_next_state(0)
+        turn(1)
+        double_y(2)
+        copy_turned(1)
+        quantise_a(1)
+        first_argument(2)
+        add_k1(0)
+        start_total(1)
 
-        for r in range(-1, ROW_TILES + 1):
+        for r in range(ROW_TILES + 1):
             if exists(r + 1):
                 subtract_next_state(r + 1)
             if exists(r):
@@ -279,8 +292,7 @@ def tile_sindylossmixin_pa_kernel(tc, x, k1, k2, coefficients, out):
                 quantise_a(r + 2)
             if exists(r + 3):
                 first_argument(r + 3)
+            if exists(r + 1):
+                add_k1(r + 1)
             if exists(r + 2):
                 start_total(r + 2)
-            if exists(r + 1):
-                add_y_and_k2(r + 1)
-                add_rest(r + 1)

@@ -252,21 +252,19 @@ def tile_sindylossmixin_pa_kernel(tc, x, k1, k2, coefficients, out):
         quantise_coefficients(0)
         turn(0)
         copy_turned(0)
+        double_y(1)
         for s in range(4, 8):
             prepare_coefficients(s)
+        double_y(2)
         quantise_a(0)
         quantise_coefficients(1)
         transposed_k3(0)
-        open_sum(0)
-        double_y(1)
-        first_argument(1)
         subtract_next_state(0)
+        first_argument(1)
         turn(1)
-        double_y(2)
         copy_turned(1)
-        quantise_a(1)
+        open_sum(0)
         first_argument(2)
-        add_k1(0)
         start_total(1)
 
         for r in range(ROW_TILES + 1):
@@ -276,6 +274,8 @@ def tile_sindylossmixin_pa_kernel(tc, x, k1, k2, coefficients, out):
                 second_argument(r)
             if exists(r - 1):
                 finish(r - 1)
+            if r == 0:
+                quantise_a(1)
             if exists(r + 2):
                 turn(r + 2)
             if exists(r + 3):
@@ -292,6 +292,8 @@ def tile_sindylossmixin_pa_kernel(tc, x, k1, k2, coefficients, out):
                 quantise_a(r + 2)
             if exists(r + 3):
                 first_argument(r + 3)
+            if r == 0:
+                add_k1(0)
             if exists(r + 1):
                 add_k1(r + 1)
             if exists(r + 2):

@@ -58,9 +58,12 @@ def tile_sindylossmixin_pa_kernel(tc, x, k1, k2, coefficients, out):
 
         c_by_slot = coefficients.rearrange("(b m j) k -> b j m k", b=HALVES, j=PACK)
         load_first_argument(0)
+        nc.sync.dma_start(out=x_next[0][:], in_=x[0, 1 : P + 1, :])
         for s in range(ROW_TILES):
             nc.sync.dma_start(out=c_rows[s][:], in_=c_by_slot[s // PACK, s % PACK])
-        for t in range(1, ROW_TILES):
+        load_first_argument(1)
+        nc.sync.dma_start(out=k1_rows[0][:], in_=k1[0:P, :])
+        for t in range(2, ROW_TILES):
             load_first_argument(t)
             load_rest(t - 1)
         load_rest(ROW_TILES - 1)
@@ -247,6 +250,7 @@ def tile_sindylossmixin_pa_kernel(tc, x, k1, k2, coefficients, out):
         double_y(0)
         start_total(0)
         first_argument(0)
+        subtract_next_state(0)
         for s in range(4):
             prepare_coefficients(s)
         quantise_coefficients(0)
@@ -259,7 +263,6 @@ def tile_sindylossmixin_pa_kernel(tc, x, k1, k2, coefficients, out):
         quantise_a(0)
         quantise_coefficients(1)
         transposed_k3(0)
-        subtract_next_state(0)
         first_argument(1)
         turn(1)
         copy_turned(1)

@@ -297,7 +297,7 @@ def tile_sindylossmixin_pa_kernel(tc, x, k1, k2, coefficients, out):
                 first_argument(r + 3)
             if r == 0:
                 add_k1(0)
-            if exists(r + 1):
-                add_k1(r + 1)
             if exists(r + 2):
                 start_total(r + 2)
+            if exists(r + 1):
+                add_k1(r + 1)

@@ -275,6 +275,9 @@ def tile_sindylossmixin_pa_kernel(tc, x, k1, k2, coefficients, out):
                 subtract_next_state(r + 1)
             if exists(r):
                 second_argument(r)
+            if r == ROW_TILES - 1:
+                quantise_b(r)
+                close_sum(r)
             if exists(r - 1):
                 finish(r - 1)
             if r == 0:
@@ -288,7 +291,7 @@ def tile_sindylossmixin_pa_kernel(tc, x, k1, k2, coefficients, out):
             if exists(r + 1):
                 transposed_k3(r + 1)
                 open_sum(r + 1)
-            if exists(r):
+            if exists(r) and r < ROW_TILES - 1:
                 quantise_b(r)
                 close_sum(r)
             if exists(r + 2):

@@ -223,6 +223,11 @@ def tile_sindylossmixin_pa_kernel(tc, x, k1, k2, coefficients, out):
                 out=total[t][:], in0=total[t][:], in1=x_next[t][:], op=SUBTRACT
             )
 
+        def subtract_next_state_on_vector(t):
+            nc.vector.tensor_tensor(
+                out=total[t][:], in0=total[t][:], in1=x_next[t][:], op=SUBTRACT
+            )
+
         def add_k1(t):
             nc.vector.scalar_tensor_tensor(
                 out=total[t][:],
@@ -271,7 +276,7 @@ def tile_sindylossmixin_pa_kernel(tc, x, k1, k2, coefficients, out):
         start_total(1)
 
         for r in range(ROW_TILES + 1):
-            if exists(r + 1):
+            if exists(r + 1) and r > 0:
                 subtract_next_state(r + 1)
             if exists(r):
                 second_argument(r)
@@ -294,6 +299,8 @@ def tile_sindylossmixin_pa_kernel(tc, x, k1, k2, coefficients, out):
             if exists(r) and r < ROW_TILES - 1:
                 quantise_b(r)
                 close_sum(r)
+            if r == 0:
+                subtract_next_state_on_vector(1)
             if exists(r + 2):
                 quantise_a(r + 2)
             if exists(r + 3):

@@ -26,6 +26,8 @@ WORDS = K_PASS // PAIR
 
 FLOPS = 2 * 2 * (ROW_TILES * P) * H * H
 
+BY_TENSOR = (2, 4, 6)
+
 
 def tile_sindylossmixin_pa_kernel(tc, x, k1, k2, coefficients, out):
     nc = tc.nc
@@ -39,6 +41,12 @@ def tile_sindylossmixin_pa_kernel(tc, x, k1, k2, coefficients, out):
 
         identity = keep.tile([P, P], F32)
         make_identity(nc, identity[:])
+        one_i = keep.tile([P, P], BF16)
+        make_identity(nc, one_i[:])
+        multiples = {1.0: one_i}
+        for factor in (6.0, -6.0, 2.0):
+            multiples[factor] = keep.tile([P, P], BF16, name="multiple_%d" % int(factor + 6))
+            nc.scalar.activation(out=multiples[factor][:], in_=one_i[:], func=COPY, scale=factor)
 
         y, x_next, k1_rows, k2_rows, c_rows = [], [], [], [], []
         for t in range(ROW_TILES):
@@ -238,6 +246,24 @@ def tile_sindylossmixin_pa_kernel(tc, x, k1, k2, coefficients, out):
                 op1=ADD,
             )
 
+        def rest_by_tensor(t, b):
+            if b == 0:
+                total[t] = work.tile([P, H], F32, name="total", bufs=6)
+            cols = slice(b * BANK, (b + 1) * BANK)
+            six_fold = turned_banks.tile([P, BANK], F32, name="turned")
+            terms = ((6.0, y[t]), (-6.0, x_next[t]), (1.0, k1_rows[t]), (2.0, k2_rows[t]))
+            for i, (factor, rows) in enumerate(terms):
+                nc.tensor.matmul(
+                    out=six_fold[:],
+                    lhsT=multiples[factor][:],
+                    rhs=rows[:, cols],
+                    start=(i == 0),
+                    stop=(i == len(terms) - 1),
+                )
+            nc.scalar.activation(
+                out=total[t][:, cols], in_=six_fold[:], func=COPY, scale=1.0 / 6.0
+            )
+
         def finish(t):
             for b in range(HALVES):
                 cols = slice(b * BANK, (b + 1) * BANK)
@@ -276,7 +302,7 @@ def tile_sindylossmixin_pa_kernel(tc, x, k1, k2, coefficients, out):
         start_total(1)
 
         for r in range(ROW_TILES + 1):
-            if exists(r + 1) and r > 0:
+            if exists(r + 1) and r > 0 and r + 1 not in BY_TENSOR:
                 subtract_next_state(r + 1)
             if exists(r):
                 second_argument(r)
@@ -289,12 +315,14 @@ def tile_sindylossmixin_pa_kernel(tc, x, k1, k2, coefficients, out):
                 quantise_a(1)
             if exists(r + 2):
                 turn(r + 2)
+                copy_turned(r + 2)
             if exists(r + 3):
                 double_y(r + 3)
-            if exists(r + 2):
-                copy_turned(r + 2)
             if exists(r + 1):
                 transposed_k3(r + 1)
+            if r // HALVES < len(BY_TENSOR):
+                rest_by_tensor(BY_TENSOR[r // HALVES], r % HALVES)
+            if exists(r + 1):
                 open_sum(r + 1)
             if exists(r) and r < ROW_TILES - 1:
                 quantise_b(r)
@@ -303,11 +331,11 @@ def tile_sindylossmixin_pa_kernel(tc, x, k1, k2, coefficients, out):
                 subtract_next_state_on_vector(1)
             if exists(r + 2):
                 quantise_a(r + 2)
-            if exists(r + 3):
-                first_argument(r + 3)
             if r == 0:
                 add_k1(0)
-            if exists(r + 2):
-                start_total(r + 2)
-            if exists(r + 1):
+            if exists(r + 1) and r + 1 not in BY_TENSOR:
                 add_k1(r + 1)
+            if exists(r + 2) and r + 2 not in BY_TENSOR:
+                start_total(r + 2)
+            if exists(r + 3):
+                first_argument(r + 3)

@@ -66,9 +66,10 @@ def tile_sindylossmixin_pa_kernel(tc, x, k1, k2, coefficients, out):
 
         c_by_slot = coefficients.rearrange("(b m j) k -> b j m k", b=HALVES, j=PACK)
         load_first_argument(0)
-        nc.sync.dma_start(out=x_next[0][:], in_=x[0, 1 : P + 1, :])
         for s in range(ROW_TILES):
             nc.sync.dma_start(out=c_rows[s][:], in_=c_by_slot[s // PACK, s % PACK])
+            if s == 0:
+                nc.sync.dma_start(out=x_next[0][:], in_=x[0, 1 : P + 1, :])
         load_first_argument(1)
         nc.sync.dma_start(out=k1_rows[0][:], in_=k1[0:P, :])
         for t in range(2, ROW_TILES):
@@ -89,6 +90,12 @@ def tile_sindylossmixin_pa_kernel(tc, x, k1, k2, coefficients, out):
                         words[:, g * WORDS + u : (g + 1) * WORDS : PAIR],
                         identity[:],
                     )
+
+        def turn_sorted_words(turned, words):
+            for g in range(PASSES):
+                for u in range(PAIR):
+                    first = u * PASSES * P + g * P
+                    nc.tensor.transpose(turned[:, g, u, :], words[:, first : first + P], identity[:])
 
         def prepare_coefficients(s):
             pool = (turned_banks, turned_banks, k3_banks, k3_banks)[s] if s < 4 else sum_banks
@@ -113,7 +120,7 @@ def tile_sindylossmixin_pa_kernel(tc, x, k1, k2, coefficients, out):
         doubled_y, doubled_a, turned_a, turned_y = {}, {}, {}, {}
         a_grouped, y_grouped, b_grouped = {}, {}, {}
         a_quantised, b_quantised = {}, {}
-        doubled_k3, total_sum, total = {}, {}, {}
+        doubled_k3, total_sum, total, y_sorted = {}, {}, {}, {}
 
         def exists(t):
             return 0 <= t < ROW_TILES
@@ -122,17 +129,27 @@ def tile_sindylossmixin_pa_kernel(tc, x, k1, k2, coefficients, out):
             doubled_y[t] = work.tile([P, H], BF16, name="doubled_y")
             nc.scalar.activation(out=doubled_y[t][:], in_=y[t][:], func=COPY, scale=2.0)
 
+        def sort_y(t):
+            y_sorted[t] = work.tile([P, H // PAIR], F32, name="y_sorted", bufs=4)
+            nc.scalar.copy(
+                out=y_sorted[t][:].rearrange("n (u q) -> n u q", u=PAIR),
+                in_=y[t][:].bitcast(F32).rearrange("n (q u) -> n u q", u=PAIR),
+            )
+
         def first_argument(t):
             doubled_a[t] = work.tile([P, H], BF16, name="doubled_a")
             nc.vector.tensor_tensor(
-                out=doubled_a[t][:], in0=doubled_y[t][:], in1=k2_rows[t][:], op=ADD
+                out=doubled_a[t][:].rearrange("n (u q e) -> n u q e", u=PAIR, e=PAIR),
+                in0=doubled_y[t][:].rearrange("n (q u e) -> n u q e", u=PAIR, e=PAIR),
+                in1=k2_rows[t][:].rearrange("n (q u e) -> n u q e", u=PAIR, e=PAIR),
+                op=ADD,
             )
 
         def turn(t):
             turned_a[t] = turned_banks.tile([P, PASSES, PAIR, P], F32, name="turned")
-            turn_words(turned_a[t], doubled_a[t])
+            turn_sorted_words(turned_a[t], doubled_a[t][:].bitcast(F32))
             turned_y[t] = turned_banks.tile([P, PASSES, PAIR, P], F32, name="turned")
-            turn_words(turned_y[t], y[t])
+            turn_sorted_words(turned_y[t], y_sorted[t][:])
 
         def as_words(grouped):
             return (
@@ -282,8 +299,11 @@ def tile_sindylossmixin_pa_kernel(tc, x, k1, k2, coefficients, out):
         start_total(0)
         first_argument(0)
         subtract_next_state(0)
-        for s in range(4):
-            prepare_coefficients(s)
+        prepare_coefficients(0)
+        prepare_coefficients(1)
+        sort_y(0)
+        prepare_coefficients(2)
+        prepare_coefficients(3)
         quantise_coefficients(0)
         turn(0)
         copy_turned(0)
@@ -291,12 +311,14 @@ def tile_sindylossmixin_pa_kernel(tc, x, k1, k2, coefficients, out):
         for s in range(4, 8):
             prepare_coefficients(s)
         double_y(2)
+        sort_y(1)
         quantise_a(0)
         quantise_coefficients(1)
         transposed_k3(0)
         first_argument(1)
         turn(1)
         copy_turned(1)
+        sort_y(2)
         open_sum(0)
         first_argument(2)
         start_total(1)
@@ -318,6 +340,7 @@ def tile_sindylossmixin_pa_kernel(tc, x, k1, k2, coefficients, out):
                 copy_turned(r + 2)
             if exists(r + 3):
                 double_y(r + 3)
+                sort_y(r + 3)
             if exists(r + 1):
                 transposed_k3(r + 1)
             if r // HALVES < len(BY_TENSOR):

@@ -26,7 +26,15 @@ WORDS = K_PASS // PAIR
 
 FLOPS = 2 * 2 * (ROW_TILES * P) * H * H
 
-BY_TENSOR = (2, 4, 6)
+BY_TENSOR = (0, 4, 7)
+TRIGGER = 16
+GP = {2: ("x", 2), 3: ("x", 3), 4: ("x", 5), 5: ("k", 5), 6: ("x", 6)}
+START = {2: (3,), 3: (5,), 5: (6,)}
+ADDK = {2: (2,), 3: (3,), 6: (6,)}
+TRIG = {4: 5}
+SCALE = {3: 5}
+REST = {2: (4, 0), 3: (4, 1), 5: (7, 0), 6: (7, 1)}
+LEAD = 4
 
 
 def tile_sindylossmixin_pa_kernel(tc, x, k1, k2, coefficients, out):
@@ -68,10 +76,8 @@ def tile_sindylossmixin_pa_kernel(tc, x, k1, k2, coefficients, out):
         load_first_argument(0)
         for s in range(ROW_TILES):
             nc.sync.dma_start(out=c_rows[s][:], in_=c_by_slot[s // PACK, s % PACK])
-            if s == 0:
-                nc.sync.dma_start(out=x_next[0][:], in_=x[0, 1 : P + 1, :])
+        load_rest(0)
         load_first_argument(1)
-        nc.sync.dma_start(out=k1_rows[0][:], in_=k1[0:P, :])
         for t in range(2, ROW_TILES):
             load_first_argument(t)
             load_rest(t - 1)
@@ -108,8 +114,8 @@ def tile_sindylossmixin_pa_kernel(tc, x, k1, k2, coefficients, out):
                 in_=turned[:].rearrange("p g u i -> p g i u"),
             )
 
-        def quantise_coefficients(b):
-            half = slice(b * BANK, (b + 1) * BANK)
+        def quantise_coefficients(first, last):
+            half = slice(first * P, last * P)
             for g in range(PASSES):
                 nc.vector.quantize_mx(
                     out=c_codes[:, g, half].bitcast(FP8X4),
@@ -120,13 +126,13 @@ def tile_sindylossmixin_pa_kernel(tc, x, k1, k2, coefficients, out):
         doubled_y, doubled_a, turned_a, turned_y = {}, {}, {}, {}
         a_grouped, y_grouped, b_grouped = {}, {}, {}
         a_quantised, b_quantised = {}, {}
-        doubled_k3, total_sum, total, y_sorted = {}, {}, {}, {}
+        doubled_k3, total_sum, total, y_sorted, k1_sixth, six_fold = {}, {}, {}, {}, {}, {}
 
         def exists(t):
             return 0 <= t < ROW_TILES
 
         def double_y(t):
-            doubled_y[t] = work.tile([P, H], BF16, name="doubled_y")
+            doubled_y[t] = work.tile([P, H], BF16, name="doubled_y", bufs=5)
             nc.scalar.activation(out=doubled_y[t][:], in_=y[t][:], func=COPY, scale=2.0)
 
         def sort_y(t):
@@ -263,22 +269,48 @@ def tile_sindylossmixin_pa_kernel(tc, x, k1, k2, coefficients, out):
                 op1=ADD,
             )
 
-        def rest_by_tensor(t, b):
-            if b == 0:
-                total[t] = work.tile([P, H], F32, name="total", bufs=6)
+        def rest_by_tensor(t, b, pool=turned_banks, label="turned"):
             cols = slice(b * BANK, (b + 1) * BANK)
-            six_fold = turned_banks.tile([P, BANK], F32, name="turned")
-            terms = ((6.0, y[t]), (-6.0, x_next[t]), (1.0, k1_rows[t]), (2.0, k2_rows[t]))
+            six_fold[t, b] = pool.tile([P, BANK], F32, name=label)
+            terms = ((6.0, y[t]), (2.0, k2_rows[t]), (-6.0, x_next[t]), (1.0, k1_rows[t]))
             for i, (factor, rows) in enumerate(terms):
                 nc.tensor.matmul(
-                    out=six_fold[:],
+                    out=six_fold[t, b][:],
                     lhsT=multiples[factor][:],
                     rhs=rows[:, cols],
                     start=(i == 0),
                     stop=(i == len(terms) - 1),
                 )
+
+        def copy_rest(t, b):
+            cols = slice(b * BANK, (b + 1) * BANK)
+            if b == 0:
+                total[t] = work.tile([P, H], F32, name="total", bufs=6)
             nc.scalar.activation(
-                out=total[t][:, cols], in_=six_fold[:], func=COPY, scale=1.0 / 6.0
+                out=total[t][:, cols], in_=six_fold[t, b][:], func=COPY, scale=1.0 / 6.0
+            )
+
+        def scale_k1(t):
+            k1_sixth[t] = work.tile([P, H], F32, name="k1_sixth", bufs=2)
+            nc.scalar.activation(
+                out=k1_sixth[t][:, : H - TRIGGER],
+                in_=k1_rows[t][:, : H - TRIGGER],
+                func=COPY,
+                scale=1.0 / 6.0,
+            )
+
+        def trigger_k1(t):
+            nc.vector.tensor_scalar(
+                out=k1_sixth[t][:, H - TRIGGER :],
+                in0=k1_rows[t][:, H - TRIGGER :],
+                scalar1=1.0 / 6.0,
+                scalar2=None,
+                op0=MULT,
+            )
+
+        def add_k1_on_gpsimd(t):
+            nc.gpsimd.tensor_tensor(
+                out=total[t][:], in0=total[t][:], in1=k1_sixth[t][:], op=ADD
             )
 
         def finish(t):
@@ -296,69 +328,101 @@ def tile_sindylossmixin_pa_kernel(tc, x, k1, k2, coefficients, out):
                 nc.sync.dma_start(out=out[t, :, cols], in_=total[t][:, cols])
 
         double_y(0)
-        start_total(0)
         first_argument(0)
-        subtract_next_state(0)
         prepare_coefficients(0)
         prepare_coefficients(1)
         sort_y(0)
         prepare_coefficients(2)
         prepare_coefficients(3)
-        quantise_coefficients(0)
+        quantise_coefficients(0, 4)
         turn(0)
         copy_turned(0)
+        prepare_coefficients(4)
+        prepare_coefficients(5)
+        prepare_coefficients(6)
+        prepare_coefficients(7)
         double_y(1)
-        for s in range(4, 8):
-            prepare_coefficients(s)
-        double_y(2)
         sort_y(1)
+        double_y(2)
+        rest_by_tensor(0, 0, sum_banks, "total_sum")
         quantise_a(0)
-        quantise_coefficients(1)
+        quantise_coefficients(4, 6)
+        quantise_coefficients(6, 8)
         transposed_k3(0)
         first_argument(1)
         turn(1)
         copy_turned(1)
         sort_y(2)
-        open_sum(0)
+        second_argument(0)
         first_argument(2)
+        rest_by_tensor(0, 1, sum_banks, "total_sum")
+        turn(2)
+        quantise_b(0)
+        quantise_a(1)
+        copy_turned(2)
+        double_y(3)
+        sort_y(3)
+        transposed_k3(1)
         start_total(1)
+        subtract_next_state_on_vector(1)
+        quantise_a(2)
+        second_argument(1)
+        copy_rest(0, 0)
+        copy_rest(0, 1)
+        open_sum(0)
+        close_sum(0)
+        double_y(4)
+        quantise_b(1)
+        first_argument(3)
+        add_k1(1)
+        transposed_k3(2)
+        turn(3)
+        copy_turned(3)
+        sort_y(4)
+        open_sum(1)
+        close_sum(1)
+        finish(0)
+        quantise_a(3)
+        start_total(2)
+        first_argument(4)
+        double_y(5)
 
-        for r in range(ROW_TILES + 1):
-            if exists(r + 1) and r > 0 and r + 1 not in BY_TENSOR:
-                subtract_next_state(r + 1)
+        for r in range(2, ROW_TILES + 1):
+            if r in GP:
+                (subtract_next_state if GP[r][0] == "x" else add_k1_on_gpsimd)(GP[r][1])
             if exists(r):
                 second_argument(r)
             if r == ROW_TILES - 1:
                 quantise_b(r)
-                close_sum(r)
             if exists(r - 1):
                 finish(r - 1)
-            if r == 0:
-                quantise_a(1)
+            if exists(r):
+                open_sum(r)
             if exists(r + 2):
                 turn(r + 2)
                 copy_turned(r + 2)
+            if exists(r + LEAD):
+                double_y(r + LEAD)
             if exists(r + 3):
-                double_y(r + 3)
                 sort_y(r + 3)
+            if r in SCALE:
+                scale_k1(SCALE[r])
             if exists(r + 1):
                 transposed_k3(r + 1)
-            if r // HALVES < len(BY_TENSOR):
-                rest_by_tensor(BY_TENSOR[r // HALVES], r % HALVES)
-            if exists(r + 1):
-                open_sum(r + 1)
-            if exists(r) and r < ROW_TILES - 1:
-                quantise_b(r)
+            if r in REST:
+                rest_by_tensor(*REST[r])
+                copy_rest(*REST[r])
+            if exists(r):
+                if r < ROW_TILES - 1:
+                    quantise_b(r)
                 close_sum(r)
-            if r == 0:
-                subtract_next_state_on_vector(1)
             if exists(r + 2):
                 quantise_a(r + 2)
-            if r == 0:
-                add_k1(0)
-            if exists(r + 1) and r + 1 not in BY_TENSOR:
-                add_k1(r + 1)
-            if exists(r + 2) and r + 2 not in BY_TENSOR:
-                start_total(r + 2)
+            for t in ADDK.get(r, ()):
+                add_k1(t)
+            for t in START.get(r, ()):
+                start_total(t)
+            if r in TRIG:
+                trigger_k1(TRIG[r])
             if exists(r + 3):
                 first_argument(r + 3)

@@ -26,15 +26,17 @@ WORDS = K_PASS // PAIR
 
 FLOPS = 2 * 2 * (ROW_TILES * P) * H * H
 
-BY_TENSOR = (0, 4, 7)
+BY_TENSOR = (0, 2, 4)
 TRIGGER = 16
-GP = {2: ("x", 2), 3: ("x", 3), 4: ("x", 5), 5: ("k", 5), 6: ("x", 6)}
-START = {2: (3,), 3: (5,), 5: (6,)}
-ADDK = {2: (2,), 3: (3,), 6: (6,)}
-TRIG = {4: 5}
-SCALE = {3: 5}
-REST = {2: (4, 0), 3: (4, 1), 5: (7, 0), 6: (7, 1)}
+FIX = 32
+GP = {2: ("x", 3), 3: ("x", 5), 4: ("x", 6), 5: ("x", 7), 6: ("k", 7)}
+START = {2: (5,), 3: (6,), 4: (7,)}
+ADDK = {2: (3,), 4: (5,), 5: (6,)}
+TRIG = {5: 7}
+SCALE = {4: (7,)}
+REST = {2: ((2, 1),), 3: ((4, 0),), 4: ((4, 1),)}
 LEAD = 4
+K2AT = 1
 
 
 def tile_sindylossmixin_pa_kernel(tc, x, k1, k2, coefficients, out):
@@ -51,15 +53,29 @@ def tile_sindylossmixin_pa_kernel(tc, x, k1, k2, coefficients, out):
         make_identity(nc, identity[:])
         one_i = keep.tile([P, P], BF16)
         make_identity(nc, one_i[:])
-        multiples = {1.0: one_i}
-        for factor in (6.0, -6.0, 2.0):
-            multiples[factor] = keep.tile([P, P], BF16, name="multiple_%d" % int(factor + 6))
-            nc.scalar.activation(out=multiples[factor][:], in_=one_i[:], func=COPY, scale=factor)
+        two_i = keep.tile([P, P], BF16)
+        nc.scalar.activation(out=two_i[:], in_=one_i[:], func=COPY, scale=2.0)
+        step_6 = keep.tile([P, P], BF16)
+        nc.gpsimd.memset(step_6[:], 0.0)
+        for below, value in ((0, 6.0), (1, -6.0)):
+            nc.gpsimd.affine_select(
+                out=step_6[:],
+                in_=step_6[:],
+                compare_op=mybir.AluOpType.not_equal,
+                fill=value,
+                base=-below,
+                pattern=[[-1, P]],
+                channel_multiplier=1,
+            )
 
-        y, x_next, k1_rows, k2_rows, c_rows = [], [], [], [], []
+        last_x = keep.tile([FIX, len(BY_TENSOR), H // FIX], BF16)
+        last_out = keep.tile([FIX, len(BY_TENSOR), H // FIX], F32)
+
+        y, x_next, k1_rows, k2_rows, c_rows = [], {}, [], [], []
         for t in range(ROW_TILES):
             y.append(keep.tile([P, H], BF16, name="y%d" % t))
-            x_next.append(keep.tile([P, H], BF16, name="x_next%d" % t))
+            if t not in BY_TENSOR:
+                x_next[t] = keep.tile([P, H], BF16, name="x_next%d" % t)
             k1_rows.append(keep.tile([P, H], BF16, name="k1_rows%d" % t))
             k2_rows.append(keep.tile([P, H], BF16, name="k2_rows%d" % t))
             c_rows.append(keep.tile([P, H], BF16, name="c_rows%d" % t))
@@ -70,12 +86,20 @@ def tile_sindylossmixin_pa_kernel(tc, x, k1, k2, coefficients, out):
 
         def load_rest(t):
             nc.sync.dma_start(out=k1_rows[t][:], in_=k1[t * P : (t + 1) * P, :])
-            nc.sync.dma_start(out=x_next[t][:], in_=x[t, 1 : P + 1, :])
+            if t in BY_TENSOR:
+                i = BY_TENSOR.index(t)
+                nc.sync.dma_start(
+                    out=last_x[:, i, :], in_=x[t, P : P + 1, :].rearrange("o (p c) -> (o p) c", p=FIX)
+                )
+            else:
+                nc.sync.dma_start(out=x_next[t][:], in_=x[t, 1 : P + 1, :])
 
         c_by_slot = coefficients.rearrange("(b m j) k -> b j m k", b=HALVES, j=PACK)
-        load_first_argument(0)
+        nc.sync.dma_start(out=y[0][:], in_=x[0, 0:P, :])
         for s in range(ROW_TILES):
             nc.sync.dma_start(out=c_rows[s][:], in_=c_by_slot[s // PACK, s % PACK])
+            if s == K2AT:
+                nc.sync.dma_start(out=k2_rows[0][:], in_=k2[0:P, :])
         load_rest(0)
         load_first_argument(1)
         for t in range(2, ROW_TILES):
@@ -151,9 +175,11 @@ def tile_sindylossmixin_pa_kernel(tc, x, k1, k2, coefficients, out):
                 op=ADD,
             )
 
-        def turn(t):
+        def turn_a(t):
             turned_a[t] = turned_banks.tile([P, PASSES, PAIR, P], F32, name="turned")
             turn_sorted_words(turned_a[t], doubled_a[t][:].bitcast(F32))
+
+        def turn_y(t):
             turned_y[t] = turned_banks.tile([P, PASSES, PAIR, P], F32, name="turned")
             turn_sorted_words(turned_y[t], y_sorted[t][:])
 
@@ -165,11 +191,21 @@ def tile_sindylossmixin_pa_kernel(tc, x, k1, k2, coefficients, out):
                 .rearrange("p (g n u) -> p g n u", g=PASSES, u=PAIR)
             )
 
+        def turn(t):
+            turn_a(t)
+            turn_y(t)
+
         def copy_turned(t):
+            copy_a(t)
+            copy_y(t)
+
+        def copy_a(t):
             a_grouped[t] = work.tile([P, PASSES, P, PACK], BF16, name="a_grouped", align_bytes=64)
             nc.scalar.copy(
                 out=as_words(a_grouped[t]), in_=turned_a[t][:].rearrange("p g u n -> p g n u")
             )
+
+        def copy_y(t):
             y_grouped[t] = work.tile([P, PASSES, P, PACK], BF16, name="y_grouped", bufs=5)
             nc.scalar.copy(
                 out=as_words(y_grouped[t]), in_=turned_y[t][:].rearrange("p g u n -> p g n u")
@@ -192,8 +228,12 @@ def tile_sindylossmixin_pa_kernel(tc, x, k1, k2, coefficients, out):
             b_quantised[t] = quantise("b", b_grouped[t])
 
         def transposed_k3(t):
-            codes, scales = a_quantised[t]
             for b in range(HALVES):
+                transposed_k3_half(t, b)
+
+        def transposed_k3_half(t, b):
+            codes, scales = a_quantised[t]
+            if True:
                 doubled_k3[t, b] = k3_banks.tile([P, PACK, P], F32, name="k3")
                 for j in range(PACK):
                     cols = slice(b * BANK + j * P, b * BANK + (j + 1) * P)
@@ -272,11 +312,11 @@ def tile_sindylossmixin_pa_kernel(tc, x, k1, k2, coefficients, out):
         def rest_by_tensor(t, b, pool=turned_banks, label="turned"):
             cols = slice(b * BANK, (b + 1) * BANK)
             six_fold[t, b] = pool.tile([P, BANK], F32, name=label)
-            terms = ((6.0, y[t]), (2.0, k2_rows[t]), (-6.0, x_next[t]), (1.0, k1_rows[t]))
-            for i, (factor, rows) in enumerate(terms):
+            terms = ((step_6, y[t]), (two_i, k2_rows[t]), (one_i, k1_rows[t]))
+            for i, (stationary, rows) in enumerate(terms):
                 nc.tensor.matmul(
                     out=six_fold[t, b][:],
-                    lhsT=multiples[factor][:],
+                    lhsT=stationary[:],
                     rhs=rows[:, cols],
                     start=(i == 0),
                     stop=(i == len(terms) - 1),
@@ -289,6 +329,18 @@ def tile_sindylossmixin_pa_kernel(tc, x, k1, k2, coefficients, out):
             nc.scalar.activation(
                 out=total[t][:, cols], in_=six_fold[t, b][:], func=COPY, scale=1.0 / 6.0
             )
+
+        def last_row(t):
+            return out[t, P - 1 : P, :].rearrange("o (p c) -> (o p) c", p=FIX)
+
+        def fetch_last_rows():
+            for i, t in enumerate(BY_TENSOR):
+                nc.sync.dma_start(out=last_out[:, i, :], in_=last_row(t))
+
+        def mend_last_rows():
+            nc.gpsimd.tensor_tensor(out=last_out[:], in0=last_out[:], in1=last_x[:], op=SUBTRACT)
+            for i, t in enumerate(BY_TENSOR):
+                nc.sync.dma_start(out=last_row(t), in_=last_out[:, i, :])
 
         def scale_k1(t):
             k1_sixth[t] = work.tile([P, H], F32, name="k1_sixth", bufs=2)
@@ -327,16 +379,19 @@ def tile_sindylossmixin_pa_kernel(tc, x, k1, k2, coefficients, out):
                 )
                 nc.sync.dma_start(out=out[t, :, cols], in_=total[t][:, cols])
 
+        sort_y(0)
         double_y(0)
-        first_argument(0)
+        turn_y(0)
         prepare_coefficients(0)
         prepare_coefficients(1)
-        sort_y(0)
+        first_argument(0)
+        copy_y(0)
         prepare_coefficients(2)
         prepare_coefficients(3)
+        turn_a(0)
+        copy_a(0)
         quantise_coefficients(0, 4)
-        turn(0)
-        copy_turned(0)
+        quantise_a(0)
         prepare_coefficients(4)
         prepare_coefficients(5)
         prepare_coefficients(6)
@@ -344,11 +399,11 @@ def tile_sindylossmixin_pa_kernel(tc, x, k1, k2, coefficients, out):
         double_y(1)
         sort_y(1)
         double_y(2)
-        rest_by_tensor(0, 0, sum_banks, "total_sum")
-        quantise_a(0)
         quantise_coefficients(4, 6)
         quantise_coefficients(6, 8)
-        transposed_k3(0)
+        transposed_k3_half(0, 0)
+        rest_by_tensor(0, 0, sum_banks, "total_sum")
+        transposed_k3_half(0, 1)
         first_argument(1)
         turn(1)
         copy_turned(1)
@@ -372,8 +427,8 @@ def tile_sindylossmixin_pa_kernel(tc, x, k1, k2, coefficients, out):
         open_sum(0)
         close_sum(0)
         double_y(4)
-        quantise_b(1)
         first_argument(3)
+        quantise_b(1)
         add_k1(1)
         transposed_k3(2)
         turn(3)
@@ -381,9 +436,11 @@ def tile_sindylossmixin_pa_kernel(tc, x, k1, k2, coefficients, out):
         sort_y(4)
         open_sum(1)
         close_sum(1)
+        rest_by_tensor(2, 0)
+        copy_rest(2, 0)
         finish(0)
         quantise_a(3)
-        start_total(2)
+        start_total(3)
         first_argument(4)
         double_y(5)
 
@@ -398,6 +455,10 @@ def tile_sindylossmixin_pa_kernel(tc, x, k1, k2, coefficients, out):
                 finish(r - 1)
             if exists(r):
                 open_sum(r)
+            if r == 6:
+                fetch_last_rows()
+            if r == 7:
+                mend_last_rows()
             if exists(r + 2):
                 turn(r + 2)
                 copy_turned(r + 2)
@@ -405,13 +466,13 @@ def tile_sindylossmixin_pa_kernel(tc, x, k1, k2, coefficients, out):
                 double_y(r + LEAD)
             if exists(r + 3):
                 sort_y(r + 3)
-            if r in SCALE:
-                scale_k1(SCALE[r])
+            for t in SCALE.get(r, ()):
+                scale_k1(t)
             if exists(r + 1):
                 transposed_k3(r + 1)
-            if r in REST:
-                rest_by_tensor(*REST[r])
-                copy_rest(*REST[r])
+            for h in REST.get(r, ()):
+                rest_by_tensor(*h)
+                copy_rest(*h)
             if exists(r):
                 if r < ROW_TILES - 1:
                     quantise_b(r)

@@ -128,8 +128,12 @@ def tile_sindylossmixin_pa_kernel(tc, x, k1, k2, coefficients, out):
                     nc.tensor.transpose(turned[:, g, u, :], words[:, first : first + P], identity[:])
 
         def prepare_coefficients(s):
-            pool = (turned_banks, turned_banks, k3_banks, k3_banks)[s] if s < 4 else sum_banks
-            label = ("turned", "turned", "k3", "k3")[s] if s < 4 else "total_sum"
+            if s in (1, 2):
+                pool, label = k3_banks, "k3"
+            elif s in (0, 7):
+                pool, label = turned_banks, "turned"
+            else:
+                pool, label = sum_banks, "total_sum"
             turned = pool.tile([P, PASSES, PAIR, P], F32, name=label)
             turn_words(turned, c_rows[s])
             copy_out = nc.vector.tensor_copy if s % 2 == 0 else nc.scalar.copy

@@ -28,6 +28,7 @@ FLOPS = 2 * 2 * (ROW_TILES * P) * H * H
 
 BY_TENSOR = (0, 2, 4)
 TRIGGER = 16
+PART = 64
 FIX = 32
 GP = {2: ("x", 3), 3: ("x", 5), 4: ("x", 6), 5: ("x", 7), 6: ("k", 7)}
 START = {2: (5,), 3: (6,), 4: (7,)}
@@ -179,8 +180,13 @@ def tile_sindylossmixin_pa_kernel(tc, x, k1, k2, coefficients, out):
                 op=ADD,
             )
 
+        def part(words):
+            nc.tensor.matmul(out=words, lhsT=one_i[:], rhs=one_i[:, :PART], start=True, stop=True)
+
         def turn_a(t):
             turned_a[t] = turned_banks.tile([P, PASSES, PAIR, P], F32, name="turned")
+            if t > 2:
+                part(turned_a[t][:, 0, 0, :PART])
             turn_sorted_words(turned_a[t], doubled_a[t][:].bitcast(F32))
 
         def turn_y(t):
@@ -239,6 +245,8 @@ def tile_sindylossmixin_pa_kernel(tc, x, k1, k2, coefficients, out):
             codes, scales = a_quantised[t]
             if True:
                 doubled_k3[t, b] = k3_banks.tile([P, PACK, P], F32, name="k3")
+                if b == 0 and t > 1:
+                    part(doubled_k3[t, b][:, 0, :PART])
                 for j in range(PACK):
                     cols = slice(b * BANK + j * P, b * BANK + (j + 1) * P)
                     for g in range(PASSES):

@@ -37,7 +37,6 @@ TRIG = {5: 7}
 SCALE = {4: (7,)}
 REST = {2: ((2, 1),), 3: ((4, 0),), 4: ((4, 1),)}
 LEAD = 4
-K2AT = 1
 
 
 def tile_sindylossmixin_pa_kernel(tc, x, k1, k2, coefficients, out):
@@ -72,41 +71,45 @@ def tile_sindylossmixin_pa_kernel(tc, x, k1, k2, coefficients, out):
         last_x = keep.tile([FIX, len(BY_TENSOR), H // FIX], BF16)
         last_out = keep.tile([FIX, len(BY_TENSOR), H // FIX], F32)
 
-        y, x_next, k1_rows, k2_rows, c_rows = [], {}, [], [], []
-        for t in range(ROW_TILES):
-            y.append(keep.tile([P, H], BF16, name="y%d" % t))
-            if t not in BY_TENSOR:
-                x_next[t] = keep.tile([P, H], BF16, name="x_next%d" % t)
-            k1_rows.append(keep.tile([P, H], BF16, name="k1_rows%d" % t))
-            k2_rows.append(keep.tile([P, H], BF16, name="k2_rows%d" % t))
-            c_rows.append(keep.tile([P, H], BF16, name="c_rows%d" % t))
+        y, x_next, k1_rows, k2_rows, c_rows = {}, {}, {}, {}, []
+        for s in range(ROW_TILES):
+            c_rows.append(keep.tile([P, H], BF16, name="c_rows%d" % s))
 
-        def load_first_argument(t):
-            nc.sync.dma_start(out=y[t][:], in_=x[t, 0:P, :])
-            nc.sync.dma_start(out=k2_rows[t][:], in_=k2[t * P : (t + 1) * P, :])
+        def load(rows, label, source, first, count):
+            together = keep.tile([P, count, H], BF16, name="%s%d" % (label, first))
+            nc.sync.dma_start(out=together[:], in_=source)
+            for i in range(count):
+                rows[first + i] = together[:, i, :]
 
-        def load_rest(t):
-            nc.sync.dma_start(out=k1_rows[t][:], in_=k1[t * P : (t + 1) * P, :])
-            if t in BY_TENSOR:
-                i = BY_TENSOR.index(t)
-                nc.sync.dma_start(
-                    out=last_x[:, i, :], in_=x[t, P : P + 1, :].rearrange("o (p c) -> (o p) c", p=FIX)
-                )
-            else:
-                nc.sync.dma_start(out=x_next[t][:], in_=x[t, 1 : P + 1, :])
+        def load_states(rows, label, start, first, count=1):
+            source = x[first : first + count, start : start + P, :].rearrange("e p h -> p e h")
+            load(rows, label, source, first, count)
+
+        def load_stage(rows, label, stage, first, count=1):
+            source = stage[first * P : (first + count) * P, :].rearrange("(e p) h -> p e h", p=P)
+            load(rows, label, source, first, count)
 
         c_by_slot = coefficients.rearrange("(b m j) k -> b j m k", b=HALVES, j=PACK)
-        nc.sync.dma_start(out=y[0][:], in_=x[0, 0:P, :])
+        load_states(y, "y", 0, 0)
         for s in range(ROW_TILES):
             nc.sync.dma_start(out=c_rows[s][:], in_=c_by_slot[s // PACK, s % PACK])
-            if s == K2AT:
-                nc.sync.dma_start(out=k2_rows[0][:], in_=k2[0:P, :])
-        load_rest(0)
-        load_first_argument(1)
-        for t in range(2, ROW_TILES):
-            load_first_argument(t)
-            load_rest(t - 1)
-        load_rest(ROW_TILES - 1)
+            if s == 1:
+                load_stage(k2_rows, "k2_rows", k2, 0)
+        load_stage(k1_rows, "k1_rows", k1, 0)
+        for t in (1, 2):
+            load_states(y, "y", 0, t)
+            load_stage(k2_rows, "k2_rows", k2, t)
+        load_stage(k1_rows, "k1_rows", k1, 1, 2)
+        load_states(x_next, "x_next", 1, 1)
+        for t, count in ((3, 2), (5, 2), (7, 1)):
+            load_states(y, "y", 0, t, count)
+            load_stage(k2_rows, "k2_rows", k2, t, count)
+            load_stage(k1_rows, "k1_rows", k1, t, count)
+            load_states(x_next, "x_next", 1, t, 1 if t == 3 else count)
+        for i, t in enumerate(BY_TENSOR):
+            nc.sync.dma_start(
+                out=last_x[:, i, :], in_=x[t, P : P + 1, :].rearrange("o (p c) -> (o p) c", p=FIX)
+            )
 
         c_grouped = keep.tile([P, PASSES, H, PAIR], F32, align_bytes=64)
         c_codes = keep.tile([P, PASSES, H], U32, align_bytes=64)
@@ -465,7 +468,7 @@ def tile_sindylossmixin_pa_kernel(tc, x, k1, k2, coefficients, out):
                 quantise_b(r)
             if exists(r - 1):
                 finish(r - 1)
-            if exists(r):
+            if exists(r) and r < ROW_TILES - 1:
                 open_sum(r)
             if r == 6:
                 fetch_last_rows()
@@ -485,17 +488,19 @@ def tile_sindylossmixin_pa_kernel(tc, x, k1, k2, coefficients, out):
             for h in REST.get(r, ()):
                 rest_by_tensor(*h)
                 copy_rest(*h)
+            if r == ROW_TILES - 2:
+                open_sum(r + 1)
             if exists(r):
                 if r < ROW_TILES - 1:
                     quantise_b(r)
                 close_sum(r)
             if exists(r + 2):
                 quantise_a(r + 2)
+            if r in TRIG:
+                trigger_k1(TRIG[r])
             for t in ADDK.get(r, ()):
                 add_k1(t)
             for t in START.get(r, ()):
                 start_total(t)
-            if r in TRIG:
-                trigger_k1(TRIG[r])
             if exists(r + 3):
                 first_argument(r + 3)

@@ -350,12 +350,12 @@ def tile_sindylossmixin_pa_kernel(tc, x, k1, k2, coefficients, out):
 
         def fetch_last_rows():
             for i, t in enumerate(BY_TENSOR):
-                nc.sync.dma_start(out=last_out[:, i, :], in_=last_row(t))
+                nc.scalar.dma_start(out=last_out[:, i, :], in_=last_row(t))
 
         def mend_last_rows():
             nc.gpsimd.tensor_tensor(out=last_out[:], in0=last_out[:], in1=last_x[:], op=SUBTRACT)
             for i, t in enumerate(BY_TENSOR):
-                nc.sync.dma_start(out=last_row(t), in_=last_out[:, i, :])
+                nc.scalar.dma_start(out=last_row(t), in_=last_out[:, i, :])
 
         def scale_k1(t):
             k1_sixth[t] = work.tile([P, H], F32, name="k1_sixth", bufs=2)

@@ -28,6 +28,10 @@ FLOPS = 2 * 2 * (ROW_TILES * P) * H * H
 
 BY_TENSOR = (0, 2, 4)
 TRIGGER = 16
+BANK_BY_BANK = tuple((b, g) for b in range(HALVES) for g in range(PASSES))
+PASS_BY_PASS = tuple((b, g) for g in range(PASSES) for b in range(HALVES))
+PIECES = ((0, BANK), (BANK, H))
+LAST_PIECES = ((0, BANK), (BANK, BANK + BANK // 2), (BANK + BANK // 2, H))
 PART = 64
 FIX = 32
 GP = {2: ("x", 3), 3: ("x", 5), 4: ("x", 6), 5: ("x", 7), 6: ("k", 7)}
@@ -36,7 +40,7 @@ ADDK = {2: (3,), 4: (5,), 5: (6,)}
 TRIG = {5: 7}
 SCALE = {4: (7,)}
 REST = {2: ((2, 1),), 3: ((4, 0),), 4: ((4, 1),)}
-LEAD = 4
+LEAD = 5
 
 
 def tile_sindylossmixin_pa_kernel(tc, x, k1, k2, coefficients, out):
@@ -164,7 +168,7 @@ def tile_sindylossmixin_pa_kernel(tc, x, k1, k2, coefficients, out):
             return 0 <= t < ROW_TILES
 
         def double_y(t):
-            doubled_y[t] = work.tile([P, H], BF16, name="doubled_y", bufs=5)
+            doubled_y[t] = work.tile([P, H], BF16, name="doubled_y", bufs=6)
             nc.scalar.activation(out=doubled_y[t][:], in_=y[t][:], func=COPY, scale=2.0)
 
         def sort_y(t):
@@ -175,7 +179,7 @@ def tile_sindylossmixin_pa_kernel(tc, x, k1, k2, coefficients, out):
             )
 
         def first_argument(t):
-            doubled_a[t] = work.tile([P, H], BF16, name="doubled_a")
+            doubled_a[t] = work.tile([P, H], BF16, name="doubled_a", bufs=5)
             nc.vector.tensor_tensor(
                 out=doubled_a[t][:].rearrange("n (u q e) -> n u q e", u=PAIR, e=PAIR),
                 in0=doubled_y[t][:].rearrange("n (q u e) -> n u q e", u=PAIR, e=PAIR),
@@ -224,21 +228,24 @@ def tile_sindylossmixin_pa_kernel(tc, x, k1, k2, coefficients, out):
                 out=as_words(y_grouped[t]), in_=turned_y[t][:].rearrange("p g u n -> p g n u")
             )
 
-        def quantise(label, grouped):
+        def quantise(label, grouped, runs=((0, PASSES),)):
             codes = work.tile([P, PASSES, P], U32, name="codes_" + label, align_bytes=64, bufs=4)
             scales = work.tile([P, PASSES, P], U8, name="scales_" + label, align_bytes=64, bufs=4)
-            nc.vector.quantize_mx(
-                out=codes[:].rearrange("p g n -> p (g n)").bitcast(FP8X4),
-                scales=scales[:].rearrange("p g n -> p (g n)"),
-                in_=grouped[:].rearrange("p g n j -> p (g n j)"),
-            )
+            for first, last in runs:
+                nc.vector.quantize_mx(
+                    out=codes[:, first:last, :].rearrange("p g n -> p (g n)").bitcast(FP8X4),
+                    scales=scales[:, first:last, :].rearrange("p g n -> p (g n)"),
+                    in_=grouped[:, first:last, :, :].rearrange("p g n j -> p (g n j)"),
+                )
             return codes, scales
 
         def quantise_a(t):
             a_quantised[t] = quantise("a", a_grouped[t])
 
         def quantise_b(t):
-            b_quantised[t] = quantise("b", b_grouped[t])
+            one_by_one = tuple((g, g + 1) for g in range(PASSES))
+            runs = one_by_one if t == ROW_TILES - 1 else ((0, PASSES),)
+            b_quantised[t] = quantise("b", b_grouped[t], runs)
 
         def transposed_k3(t):
             for b in range(HALVES):
@@ -263,28 +270,28 @@ def tile_sindylossmixin_pa_kernel(tc, x, k1, k2, coefficients, out):
                             stop=(g == PASSES - 1),
                         )
 
-        def times_coefficients(t, quantised, first, last):
+        def times_coefficients(t, quantised, first, last, order):
             codes, scales = quantised
-            for b in range(HALVES):
+            for b, g in order:
                 cols = slice(b * BANK, (b + 1) * BANK)
-                for g in range(PASSES):
-                    nc.tensor.matmul_mx(
-                        out=total_sum[t, b][:],
-                        lhsT=codes[:, g, :].bitcast(FP8X4),
-                        lhsT_scale=scales[:, g, :],
-                        rhs=c_codes[:, g, cols].bitcast(FP8X4),
-                        rhs_scale=c_scales[:, g, cols],
-                        start=(first and g == 0),
-                        stop=(last and g == PASSES - 1),
-                    )
+                nc.tensor.matmul_mx(
+                    out=total_sum[t, b][:],
+                    lhsT=codes[:, g, :].bitcast(FP8X4),
+                    lhsT_scale=scales[:, g, :],
+                    rhs=c_codes[:, g, cols].bitcast(FP8X4),
+                    rhs_scale=c_scales[:, g, cols],
+                    start=(first and g == 0),
+                    stop=(last and g == PASSES - 1),
+                )
 
         def open_sum(t):
             for b in range(HALVES):
                 total_sum[t, b] = sum_banks.tile([P, BANK], F32, name="total_sum")
-            times_coefficients(t, a_quantised[t], True, False)
+            times_coefficients(t, a_quantised[t], True, False, BANK_BY_BANK)
 
         def close_sum(t):
-            times_coefficients(t, b_quantised[t], False, True)
+            order = PASS_BY_PASS if t == ROW_TILES - 1 else BANK_BY_BANK
+            times_coefficients(t, b_quantised[t], False, True, order)
 
         def second_argument(t):
             b_grouped[t] = work.tile([P, PASSES, P, PACK], BF16, name="b_grouped", align_bytes=64)
@@ -298,10 +305,16 @@ def tile_sindylossmixin_pa_kernel(tc, x, k1, k2, coefficients, out):
                     op1=ADD,
                 )
 
-        def start_total(t):
-            total[t] = work.tile([P, H], F32, name="total", bufs=6)
+        def start_total(t, cols=slice(0, H)):
+            if cols.start == 0:
+                total[t] = work.tile([P, H], F32, name="total", bufs=6)
             nc.vector.scalar_tensor_tensor(
-                out=total[t][:], in0=k2_rows[t][:], scalar=1.0 / 3.0, in1=y[t][:], op0=MULT, op1=ADD
+                out=total[t][:, cols],
+                in0=k2_rows[t][:, cols],
+                scalar=1.0 / 3.0,
+                in1=y[t][:, cols],
+                op0=MULT,
+                op1=ADD,
             )
 
         def subtract_next_state(t):
@@ -381,12 +394,13 @@ def tile_sindylossmixin_pa_kernel(tc, x, k1, k2, coefficients, out):
             )
 
         def finish(t):
-            for b in range(HALVES):
-                cols = slice(b * BANK, (b + 1) * BANK)
+            for first, last in LAST_PIECES if t == ROW_TILES - 1 else PIECES:
+                b, cols = first // BANK, slice(first, last)
+                within = slice((first - b * BANK) // PACK, (last - b * BANK) // PACK)
                 natural = total[t][:, cols].rearrange("n (m j) -> n m j", j=PACK)
                 nc.vector.scalar_tensor_tensor(
                     out=natural,
-                    in0=total_sum[t, b][:].rearrange("n (j m) -> n m j", j=PACK),
+                    in0=total_sum[t, b][:].rearrange("n (j m) -> n m j", j=PACK)[:, within, :],
                     scalar=1.0 / 6.0,
                     in1=natural,
                     op0=MULT,
@@ -426,16 +440,18 @@ def tile_sindylossmixin_pa_kernel(tc, x, k1, k2, coefficients, out):
         second_argument(0)
         first_argument(2)
         rest_by_tensor(0, 1, sum_banks, "total_sum")
-        turn(2)
+        turn_a(2)
         quantise_b(0)
         quantise_a(1)
-        copy_turned(2)
-        double_y(3)
-        sort_y(3)
+        copy_a(2)
         transposed_k3(1)
+        turn_y(2)
+        double_y(3)
+        copy_y(2)
+        sort_y(3)
         start_total(1)
-        subtract_next_state_on_vector(1)
         quantise_a(2)
+        subtract_next_state_on_vector(1)
         second_argument(1)
         copy_rest(0, 0)
         copy_rest(0, 1)
@@ -444,20 +460,22 @@ def tile_sindylossmixin_pa_kernel(tc, x, k1, k2, coefficients, out):
         double_y(4)
         first_argument(3)
         quantise_b(1)
-        add_k1(1)
         transposed_k3(2)
         turn(3)
         copy_turned(3)
+        double_y(5)
         sort_y(4)
         open_sum(1)
         close_sum(1)
         rest_by_tensor(2, 0)
         copy_rest(2, 0)
         finish(0)
+        add_k1(1)
+        first_argument(4)
         quantise_a(3)
         start_total(3)
-        first_argument(4)
-        double_y(5)
+        first_argument(5)
+        double_y(6)
 
         for r in range(2, ROW_TILES + 1):
             if r in GP:
@@ -502,5 +520,5 @@ def tile_sindylossmixin_pa_kernel(tc, x, k1, k2, coefficients, out):
                 add_k1(t)
             for t in START.get(r, ()):
                 start_total(t)
-            if exists(r + 3):
-                first_argument(r + 3)
+            if exists(r + 4):
+                first_argument(r + 4)

from contextlib import ExitStack

import concourse.mybir as mybir
from concourse.masks import make_identity

BF16 = mybir.dt.bfloat16
F32 = mybir.dt.float32
U32 = mybir.dt.uint32
U8 = mybir.dt.uint8
FP8X4 = mybir.dt.float8_e4m3fn_x4
ADD = mybir.AluOpType.add
SUBTRACT = mybir.AluOpType.subtract
MULT = mybir.AluOpType.mult
COPY = mybir.ActivationFunctionType.Copy

P = 128
PACK = 4
PAIR = 2
K_PASS = P * PACK
H = 1024
PASSES = H // K_PASS
BANK = 512
HALVES = H // BANK
ROW_TILES = 8
WORDS = K_PASS // PAIR

FLOPS = 2 * 2 * (ROW_TILES * P) * H * H

BY_TENSOR = (0, 2, 4)
TRIGGER = 16
BANK_BY_BANK = tuple((b, g) for b in range(HALVES) for g in range(PASSES))
PASS_BY_PASS = tuple((b, g) for g in range(PASSES) for b in range(HALVES))
PIECES = ((0, BANK), (BANK, H))
LAST_PIECES = ((0, BANK), (BANK, BANK + BANK // 2), (BANK + BANK // 2, H))
PART = 64
FIX = 32
GP = {2: ("x", 3), 3: ("x", 5), 4: ("x", 6), 5: ("x", 7), 6: ("k", 7)}
START = {2: (5,), 3: (6,), 4: (7,)}
ADDK = {2: (3,), 4: (5,), 5: (6,)}
TRIG = {5: 7}
SCALE = {4: (7,)}
REST = {2: ((2, 1),), 3: ((4, 0),), 4: ((4, 1),)}
LEAD = 5


def tile_sindylossmixin_pa_kernel(tc, x, k1, k2, coefficients, out):
    nc = tc.nc
    with ExitStack() as stack:
        stack.enter_context(tc.manual_schedule())
        keep = stack.enter_context(tc.tile_pool(name="keep", bufs=1))
        work = stack.enter_context(tc.tile_pool(name="work", bufs=3))
        turned_banks = stack.enter_context(tc.psum_pool(name="turned_banks", bufs=2))
        k3_banks = stack.enter_context(tc.psum_pool(name="k3_banks", bufs=2))
        sum_banks = stack.enter_context(tc.psum_pool(name="sum_banks", bufs=4))

        identity = keep.tile([P, P], F32)
        make_identity(nc, identity[:])
        one_i = keep.tile([P, P], BF16)
        make_identity(nc, one_i[:])
        two_i = keep.tile([P, P], BF16)
        nc.scalar.activation(out=two_i[:], in_=one_i[:], func=COPY, scale=2.0)
        step_6 = keep.tile([P, P], BF16)
        nc.gpsimd.memset(step_6[:], 0.0)
        for below, value in ((0, 6.0), (1, -6.0)):
            nc.gpsimd.affine_select(
                out=step_6[:],
                in_=step_6[:],
                compare_op=mybir.AluOpType.not_equal,
                fill=value,
                base=-below,
                pattern=[[-1, P]],
                channel_multiplier=1,
            )

        last_x = keep.tile([FIX, len(BY_TENSOR), H // FIX], BF16)
        last_out = keep.tile([FIX, len(BY_TENSOR), H // FIX], F32)

        y, x_next, k1_rows, k2_rows, c_rows = {}, {}, {}, {}, []
        for s in range(ROW_TILES):
            c_rows.append(keep.tile([P, H], BF16, name="c_rows%d" % s))

        def load(rows, label, source, first, count):
            together = keep.tile([P, count, H], BF16, name="%s%d" % (label, first))
            nc.sync.dma_start(out=together[:], in_=source)
            for i in range(count):
                rows[first + i] = together[:, i, :]

        def load_states(rows, label, start, first, count=1):
            source = x[first : first + count, start : start + P, :].rearrange("e p h -> p e h")
            load(rows, label, source, first, count)

        def load_stage(rows, label, stage, first, count=1):
            source = stage[first * P : (first + count) * P, :].rearrange("(e p) h -> p e h", p=P)
            load(rows, label, source, first, count)

        c_by_slot = coefficients.rearrange("(b m j) k -> b j m k", b=HALVES, j=PACK)
        load_states(y, "y", 0, 0)
        for s in range(ROW_TILES):
            nc.sync.dma_start(out=c_rows[s][:], in_=c_by_slot[s // PACK, s % PACK])
            if s == 1:
                load_stage(k2_rows, "k2_rows", k2, 0)
        load_stage(k1_rows, "k1_rows", k1, 0)
        for t in (1, 2):
            load_states(y, "y", 0, t)
            load_stage(k2_rows, "k2_rows", k2, t)
        load_stage(k1_rows, "k1_rows", k1, 1, 2)
        load_states(x_next, "x_next", 1, 1)
        for t, count in ((3, 2), (5, 2), (7, 1)):
            load_states(y, "y", 0, t, count)
            load_stage(k2_rows, "k2_rows", k2, t, count)
            load_stage(k1_rows, "k1_rows", k1, t, count)
            load_states(x_next, "x_next", 1, t, 1 if t == 3 else count)
        for i, t in enumerate(BY_TENSOR):
            nc.sync.dma_start(
                out=last_x[:, i, :], in_=x[t, P : P + 1, :].rearrange("o (p c) -> (o p) c", p=FIX)
            )

        c_grouped = keep.tile([P, PASSES, H, PAIR], F32, align_bytes=64)
        c_codes = keep.tile([P, PASSES, H], U32, align_bytes=64)
        c_scales = keep.tile([P, PASSES, H], U8, align_bytes=64)

        def turn_words(turned, rows):
            words = rows[:].bitcast(F32)
            for g in range(PASSES):
                for u in range(PAIR):
                    nc.tensor.transpose(
                        turned[:, g, u, :],
                        words[:, g * WORDS + u : (g + 1) * WORDS : PAIR],
                        identity[:],
                    )

        def turn_sorted_words(turned, words):
            for g in range(PASSES):
                for u in range(PAIR):
                    first = u * PASSES * P + g * P
                    nc.tensor.transpose(turned[:, g, u, :], words[:, first : first + P], identity[:])

        def prepare_coefficients(s):
            if s in (1, 2):
                pool, label = k3_banks, "k3"
            elif s in (0, 7):
                pool, label = turned_banks, "turned"
            else:
                pool, label = sum_banks, "total_sum"
            turned = pool.tile([P, PASSES, PAIR, P], F32, name=label)
            turn_words(turned, c_rows[s])
            copy_out = nc.vector.tensor_copy if s % 2 == 0 else nc.scalar.copy
            copy_out(
                out=c_grouped[:, :, s * P : (s + 1) * P, :],
                in_=turned[:].rearrange("p g u i -> p g i u"),
            )

        def quantise_coefficients(first, last):
            half = slice(first * P, last * P)
            for g in range(PASSES):
                nc.vector.quantize_mx(
                    out=c_codes[:, g, half].bitcast(FP8X4),
                    scales=c_scales[:, g, half],
                    in_=c_grouped[:, g, half, :].rearrange("p i u -> p (i u)").bitcast(BF16),
                )

        doubled_y, doubled_a, turned_a, turned_y = {}, {}, {}, {}
        a_grouped, y_grouped, b_grouped = {}, {}, {}
        a_quantised, b_quantised = {}, {}
        doubled_k3, total_sum, total, y_sorted, k1_sixth, six_fold = {}, {}, {}, {}, {}, {}

        def exists(t):
            return 0 <= t < ROW_TILES

        def double_y(t):
            doubled_y[t] = work.tile([P, H], BF16, name="doubled_y", bufs=6)
            nc.scalar.activation(out=doubled_y[t][:], in_=y[t][:], func=COPY, scale=2.0)

        def sort_y(t):
            y_sorted[t] = work.tile([P, H // PAIR], F32, name="y_sorted", bufs=4)
            nc.scalar.copy(
                out=y_sorted[t][:].rearrange("n (u q) -> n u q", u=PAIR),
                in_=y[t][:].bitcast(F32).rearrange("n (q u) -> n u q", u=PAIR),
            )

        def first_argument(t):
            doubled_a[t] = work.tile([P, H], BF16, name="doubled_a", bufs=5)
            nc.vector.tensor_tensor(
                out=doubled_a[t][:].rearrange("n (u q e) -> n u q e", u=PAIR, e=PAIR),
                in0=doubled_y[t][:].rearrange("n (q u e) -> n u q e", u=PAIR, e=PAIR),
                in1=k2_rows[t][:].rearrange("n (q u e) -> n u q e", u=PAIR, e=PAIR),
                op=ADD,
            )

        def part(words):
            nc.tensor.matmul(out=words, lhsT=one_i[:], rhs=one_i[:, :PART], start=True, stop=True)

        def turn_a(t):
            turned_a[t] = turned_banks.tile([P, PASSES, PAIR, P], F32, name="turned")
            if t > 2:
                part(turned_a[t][:, 0, 0, :PART])
            turn_sorted_words(turned_a[t], doubled_a[t][:].bitcast(F32))

        def turn_y(t):
            turned_y[t] = turned_banks.tile([P, PASSES, PAIR, P], F32, name="turned")
            turn_sorted_words(turned_y[t], y_sorted[t][:])

        def as_words(grouped):
            return (
                grouped[:]
                .rearrange("p g n j -> p (g n j)")
                .bitcast(F32)
                .rearrange("p (g n u) -> p g n u", g=PASSES, u=PAIR)
            )

        def turn(t):
            turn_a(t)
            turn_y(t)

        def copy_turned(t):
            copy_a(t)
            copy_y(t)

        def copy_a(t):
            a_grouped[t] = work.tile([P, PASSES, P, PACK], BF16, name="a_grouped", align_bytes=64)
            nc.scalar.copy(
                out=as_words(a_grouped[t]), in_=turned_a[t][:].rearrange("p g u n -> p g n u")
            )

        def copy_y(t):
            y_grouped[t] = work.tile([P, PASSES, P, PACK], BF16, name="y_grouped", bufs=5)
            nc.scalar.copy(
                out=as_words(y_grouped[t]), in_=turned_y[t][:].rearrange("p g u n -> p g n u")
            )

        def quantise(label, grouped, runs=((0, PASSES),)):
            codes = work.tile([P, PASSES, P], U32, name="codes_" + label, align_bytes=64, bufs=4)
            scales = work.tile([P, PASSES, P], U8, name="scales_" + label, align_bytes=64, bufs=4)
            for first, last in runs:
                nc.vector.quantize_mx(
                    out=codes[:, first:last, :].rearrange("p g n -> p (g n)").bitcast(FP8X4),
                    scales=scales[:, first:last, :].rearrange("p g n -> p (g n)"),
                    in_=grouped[:, first:last, :, :].rearrange("p g n j -> p (g n j)"),
                )
            return codes, scales

        def quantise_a(t):
            a_quantised[t] = quantise("a", a_grouped[t])

        def quantise_b(t):
            one_by_one = tuple((g, g + 1) for g in range(PASSES))
            runs = one_by_one if t == ROW_TILES - 1 else ((0, PASSES),)
            b_quantised[t] = quantise("b", b_grouped[t], runs)

        def transposed_k3(t):
            for b in range(HALVES):
                transposed_k3_half(t, b)

        def transposed_k3_half(t, b):
            codes, scales = a_quantised[t]
            if True:
                doubled_k3[t, b] = k3_banks.tile([P, PACK, P], F32, name="k3")
                if b == 0 and t > 1:
                    part(doubled_k3[t, b][:, 0, :PART])
                for j in range(PACK):
                    cols = slice(b * BANK + j * P, b * BANK + (j + 1) * P)
                    for g in range(PASSES):
                        nc.tensor.matmul_mx(
                            out=doubled_k3[t, b][:, j, :],
                            lhsT=c_codes[:, g, cols].bitcast(FP8X4),
                            lhsT_scale=c_scales[:, g, cols],
                            rhs=codes[:, g, :].bitcast(FP8X4),
                            rhs_scale=scales[:, g, :],
                            start=(g == 0),
                            stop=(g == PASSES - 1),
                        )

        def times_coefficients(t, quantised, first, last, order):
            codes, scales = quantised
            for b, g in order:
                cols = slice(b * BANK, (b + 1) * BANK)
                nc.tensor.matmul_mx(
                    out=total_sum[t, b][:],
                    lhsT=codes[:, g, :].bitcast(FP8X4),
                    lhsT_scale=scales[:, g, :],
                    rhs=c_codes[:, g, cols].bitcast(FP8X4),
                    rhs_scale=c_scales[:, g, cols],
                    start=(first and g == 0),
                    stop=(last and g == PASSES - 1),
                )

        def open_sum(t):
            for b in range(HALVES):
                total_sum[t, b] = sum_banks.tile([P, BANK], F32, name="total_sum")
            times_coefficients(t, a_quantised[t], True, False, BANK_BY_BANK)

        def close_sum(t):
            order = PASS_BY_PASS if t == ROW_TILES - 1 else BANK_BY_BANK
            times_coefficients(t, b_quantised[t], False, True, order)

        def second_argument(t):
            b_grouped[t] = work.tile([P, PASSES, P, PACK], BF16, name="b_grouped", align_bytes=64)
            for b in range(HALVES):
                nc.vector.scalar_tensor_tensor(
                    out=b_grouped[t][:, b, :, :],
                    in0=doubled_k3[t, b][:].rearrange("p j n -> p n j"),
                    scalar=0.5,
                    in1=y_grouped[t][:, b, :, :],
                    op0=MULT,
                    op1=ADD,
                )

        def start_total(t, cols=slice(0, H)):
            if cols.start == 0:
                total[t] = work.tile([P, H], F32, name="total", bufs=6)
            nc.vector.scalar_tensor_tensor(
                out=total[t][:, cols],
                in0=k2_rows[t][:, cols],
                scalar=1.0 / 3.0,
                in1=y[t][:, cols],
                op0=MULT,
                op1=ADD,
            )

        def subtract_next_state(t):
            nc.gpsimd.tensor_tensor(
                out=total[t][:], in0=total[t][:], in1=x_next[t][:], op=SUBTRACT
            )

        def subtract_next_state_on_vector(t):
            nc.vector.tensor_tensor(
                out=total[t][:], in0=total[t][:], in1=x_next[t][:], op=SUBTRACT
            )

        def add_k1(t):
            nc.vector.scalar_tensor_tensor(
                out=total[t][:],
                in0=k1_rows[t][:],
                scalar=1.0 / 6.0,
                in1=total[t][:],
                op0=MULT,
                op1=ADD,
            )

        def rest_by_tensor(t, b, pool=turned_banks, label="turned"):
            cols = slice(b * BANK, (b + 1) * BANK)
            six_fold[t, b] = pool.tile([P, BANK], F32, name=label)
            terms = ((step_6, y[t]), (two_i, k2_rows[t]), (one_i, k1_rows[t]))
            for i, (stationary, rows) in enumerate(terms):
                nc.tensor.matmul(
                    out=six_fold[t, b][:],
                    lhsT=stationary[:],
                    rhs=rows[:, cols],
                    start=(i == 0),
                    stop=(i == len(terms) - 1),
                )

        def copy_rest(t, b):
            cols = slice(b * BANK, (b + 1) * BANK)
            if b == 0:
                total[t] = work.tile([P, H], F32, name="total", bufs=6)
            nc.scalar.activation(
                out=total[t][:, cols], in_=six_fold[t, b][:], func=COPY, scale=1.0 / 6.0
            )

        def last_row(t):
            return out[t, P - 1 : P, :].rearrange("o (p c) -> (o p) c", p=FIX)

        def fetch_last_rows():
            for i, t in enumerate(BY_TENSOR):
                nc.scalar.dma_start(out=last_out[:, i, :], in_=last_row(t))

        def mend_last_rows():
            nc.gpsimd.tensor_tensor(out=last_out[:], in0=last_out[:], in1=last_x[:], op=SUBTRACT)
            for i, t in enumerate(BY_TENSOR):
                nc.scalar.dma_start(out=last_row(t), in_=last_out[:, i, :])

        def scale_k1(t):
            k1_sixth[t] = work.tile([P, H], F32, name="k1_sixth", bufs=2)
            nc.scalar.activation(
                out=k1_sixth[t][:, : H - TRIGGER],
                in_=k1_rows[t][:, : H - TRIGGER],
                func=COPY,
                scale=1.0 / 6.0,
            )

        def trigger_k1(t):
            nc.vector.tensor_scalar(
                out=k1_sixth[t][:, H - TRIGGER :],
                in0=k1_rows[t][:, H - TRIGGER :],
                scalar1=1.0 / 6.0,
                scalar2=None,
                op0=MULT,
            )

        def add_k1_on_gpsimd(t):
            nc.gpsimd.tensor_tensor(
                out=total[t][:], in0=total[t][:], in1=k1_sixth[t][:], op=ADD
            )

        def finish(t):
            for first, last in LAST_PIECES if t == ROW_TILES - 1 else PIECES:
                b, cols = first // BANK, slice(first, last)
                within = slice((first - b * BANK) // PACK, (last - b * BANK) // PACK)
                natural = total[t][:, cols].rearrange("n (m j) -> n m j", j=PACK)
                nc.vector.scalar_tensor_tensor(
                    out=natural,
                    in0=total_sum[t, b][:].rearrange("n (j m) -> n m j", j=PACK)[:, within, :],
                    scalar=1.0 / 6.0,
                    in1=natural,
                    op0=MULT,
                    op1=ADD,
                )
                nc.sync.dma_start(out=out[t, :, cols], in_=total[t][:, cols])

        sort_y(0)
        double_y(0)
        turn_y(0)
        prepare_coefficients(0)
        prepare_coefficients(1)
        first_argument(0)
        copy_y(0)
        prepare_coefficients(2)
        prepare_coefficients(3)
        turn_a(0)
        copy_a(0)
        quantise_coefficients(0, 4)
        quantise_a(0)
        prepare_coefficients(4)
        prepare_coefficients(5)
        prepare_coefficients(6)
        prepare_coefficients(7)
        double_y(1)
        sort_y(1)
        double_y(2)
        quantise_coefficients(4, 6)
        quantise_coefficients(6, 8)
        transposed_k3_half(0, 0)
        rest_by_tensor(0, 0, sum_banks, "total_sum")
        transposed_k3_half(0, 1)
        first_argument(1)
        turn(1)
        copy_turned(1)
        sort_y(2)
        second_argument(0)
        first_argument(2)
        rest_by_tensor(0, 1, sum_banks, "total_sum")
        turn_a(2)
        quantise_b(0)
        quantise_a(1)
        copy_a(2)
        transposed_k3(1)
        turn_y(2)
        double_y(3)
        copy_y(2)
        sort_y(3)
        start_total(1)
        quantise_a(2)
        subtract_next_state_on_vector(1)
        second_argument(1)
        copy_rest(0, 0)
        copy_rest(0, 1)
        open_sum(0)
        close_sum(0)
        double_y(4)
        first_argument(3)
        quantise_b(1)
        transposed_k3(2)
        turn(3)
        copy_turned(3)
        double_y(5)
        sort_y(4)
        open_sum(1)
        close_sum(1)
        rest_by_tensor(2, 0)
        copy_rest(2, 0)
        finish(0)
        add_k1(1)
        first_argument(4)
        quantise_a(3)
        start_total(3)
        first_argument(5)
        double_y(6)

        for r in range(2, ROW_TILES + 1):
            if r in GP:
                (subtract_next_state if GP[r][0] == "x" else add_k1_on_gpsimd)(GP[r][1])
            if exists(r):
                second_argument(r)
            if r == ROW_TILES - 1:
                quantise_b(r)
            if exists(r - 1):
                finish(r - 1)
            if exists(r) and r < ROW_TILES - 1:
                open_sum(r)
            if r == 6:
                fetch_last_rows()
            if r == 7:
                mend_last_rows()
            if exists(r + 2):
                turn(r + 2)
                copy_turned(r + 2)
            if exists(r + LEAD):
                double_y(r + LEAD)
            if exists(r + 3):
                sort_y(r + 3)
            for t in SCALE.get(r, ()):
                scale_k1(t)
            if exists(r + 1):
                transposed_k3(r + 1)
            for h in REST.get(r, ()):
                rest_by_tensor(*h)
                copy_rest(*h)
            if r == ROW_TILES - 2:
                open_sum(r + 1)
            if exists(r):
                if r < ROW_TILES - 1:
                    quantise_b(r)
                close_sum(r)
            if exists(r + 2):
                quantise_a(r + 2)
            if r in TRIG:
                trigger_k1(TRIG[r])
            for t in ADDK.get(r, ()):
                add_k1(t)
            for t in START.get(r, ()):
                start_total(t)
            if exists(r + 4):
                first_argument(r + 4)
